import numpy as np
import ml_dtypes


def mxq(x, axis, fmt="e4m3"):
    dtype, down = {"e4m3": (ml_dtypes.float8_e4m3fn, 7), "e5m2": (ml_dtypes.float8_e5m2, 14)}[fmt]
    v = np.moveaxis(np.asarray(x, np.float32).astype(ml_dtypes.bfloat16).astype(np.float64), axis, -1)
    blocks = v.reshape(v.shape[:-1] + (-1, 32))
    amax = np.abs(blocks).max(-1, keepdims=True)
    byte = np.maximum(np.where(amax > 0, np.frexp(amax)[1] - 1 + 127, 0) - down, 1)
    scale = np.exp2(byte - 127.0)
    codes = (blocks / scale).astype(np.float32).astype(dtype).astype(np.float64)
    return np.moveaxis((codes * scale).reshape(v.shape), -1, axis)


WIDE = False


def mx_kscale(k):
    if not WIDE:
        return np.ones(k)
    levels = np.array([10, -10, 5, -5, 0])
    a = np.random.permutation(np.resize(levels, k // 512 * 4)).reshape(k // 512, 4)
    idx = np.arange(k)
    return np.exp2(a[idx // 512, idx % 128 // 32])


BF16 = ml_dtypes.bfloat16


def bf(x):
    return np.asarray(x, np.float32).astype(BF16)


def f64(x):
    return np.asarray(x).astype(np.float64)


N1, N2, D = 2048, 4096, 512
NB = N2 // 2
MIN_VARIANCE = 0.1
W_MEAN = 1.0
W_DIST = 1.0
W_DISP = 1.0


def setup_inputs():
    s = mx_kscale(D)
    w = s / s.min()
    g = 0.1 + 0.4 * np.random.random(D)
    mu = 0.25 * np.random.standard_normal(D)
    off = 0.8 * np.random.standard_normal(D)
    base = mu + g * np.random.standard_normal((NB, D))
    far = mu + off + g * np.random.standard_normal((N2 - NB, D))
    sgn = np.sign(np.random.standard_normal(D))
    far[-2] = sgn * w
    far[-1] = -sgn * w
    c2 = np.concatenate([base, far], axis=0)[np.random.permutation(N2)]
    c1 = base[np.random.randint(0, NB, N1)] + 0.9 / np.sqrt(D) * np.random.standard_normal((N1, D))
    return {"cluster1": bf(c1), "cluster2": bf(c2)}


def _mean_loss(c1, c2):
    m1 = np.mean(c1, axis=0)
    m2 = np.mean(c2, axis=0)
    return np.mean((m1 - m2) ** 2)


def _distance_loss(c1, c2):
    sq1 = np.sum(c1 * c1, axis=1)
    sq2 = np.sum(c2 * c2, axis=1)
    cross = mxq(c1, 1, "e4m3") @ mxq(c2, 1, "e4m3").T
    d2 = sq1[:, None] - 2.0 * cross + sq2[None, :]
    return np.mean(np.min(d2, axis=1))


def _dispersion_loss(c, min_variance=MIN_VARIANCE):
    mean = np.mean(c, axis=0)
    variances = np.mean((c - mean) ** 2, axis=0)
    return np.mean(np.maximum(min_variance - variances, 0.0))


def reference(cluster1, cluster2):
    c1 = f64(cluster1)
    c2 = f64(cluster2)
    return (W_MEAN * _mean_loss(c1, c2)
            + W_DIST * _distance_loss(c1, c2)
            + W_DISP * _dispersion_loss(c1))

@@ -1,0 +1,301 @@
+from contextlib import ExitStack
+
+import concourse.mybir as mybir
+from concourse.masks import make_identity
+
+F32 = mybir.dt.float32
+BF16 = mybir.dt.bfloat16
+U32 = mybir.dt.uint32
+U8 = mybir.dt.uint8
+FP8X4 = mybir.dt.float8_e4m3fn_x4
+ALU = mybir.AluOpType
+ACT = mybir.ActivationFunctionType
+AX = mybir.AxisListType
+
+P = 128
+N1, N2, D = 2048, 4096, 512
+CH = 512
+TPC = CH // P
+NCH1 = N1 // CH
+NCH2 = N2 // CH
+NT1 = N1 // P
+NT2 = N2 // P
+FLOPS = 2 * N1 * N2 * D
+
+
+def tile_customloss_kernel(tc, cluster1, cluster2, out):
+    nc = tc.nc
+    with ExitStack() as ctx:
+        keep = ctx.enter_context(tc.tile_pool(name="keep", bufs=1))
+        scrap = ctx.enter_context(tc.tile_pool(name="scrap", bufs=2))
+        ps_ring = ctx.enter_context(tc.psum_pool(name="ps_ring", bufs=6))
+        ps_sm = ctx.enter_context(tc.psum_pool(name="ps_sm", bufs=1))
+        ctx.enter_context(tc.manual_schedule())
+
+        x1 = keep.tile([P, NT1, D], BF16)
+        x2 = keep.tile([P, NT2, D], BF16)
+        g1 = keep.tile([P, N1, 4], BF16, align_bytes=64)
+        g2 = keep.tile([P, N2, 4], BF16, align_bytes=64)
+        codes1 = keep.tile([P, N1], U32, align_bytes=64)
+        codes2 = keep.tile([P, N2], U32, align_bytes=64)
+        scales1 = keep.tile([P, N1], U8, align_bytes=64)
+        scales2 = keep.tile([P, N2], U8, align_bytes=64)
+        acc = keep.tile([P, N1], F32)
+        ident = keep.tile([P, P], F32)
+        ones = keep.tile([P, 2], BF16)
+        sq2 = keep.tile([P, NT2], F32)
+        half2 = keep.tile([P, NT2], F32)
+        last = keep.tile([P, P], F32)
+        m1 = keep.tile([P, 4], F32)
+        negm1 = keep.tile([P, 4], F32)
+        m2 = keep.tile([P, 4], F32)
+        dev = keep.tile([P, 4], F32)
+        junkv = keep.tile([P, N1], BF16)
+        diff = keep.tile([P, 4], F32)
+        parts = keep.tile([P, 4], F32)
+        junks = keep.tile([P, 4], F32)
+        sum_a = keep.tile([P, 1], F32)
+        sum_b = keep.tile([P, 1], F32)
+        rest = keep.tile([P, 1], F32)
+        best = keep.tile([P, NT1], F32)
+        total = keep.tile([P, 1], F32)
+        res = keep.tile([P, 1], F32)
+        sums = ps_sm.tile([P, 8, 2], F32, tag="sums")
+
+        make_identity(nc, ident[:])
+        nc.vector.memset(ones[:], 1.0)
+        nc.vector.memset(last[:], 0.0)
+
+        def load(x, src, c):
+            nc.sync.dma_start(
+                out=x[:, TPC * c : TPC * (c + 1), :],
+                in_=src[CH * c : CH * (c + 1), :].rearrange("(p t) k -> p t k", t=TPC),
+            )
+
+        load(x1, cluster1, 0)
+        load(x2, cluster2, 0)
+        for c in range(1, NCH1):
+            load(x1, cluster1, c)
+        for c in range(1, NCH2):
+            load(x2, cluster2, c)
+
+        side1 = (x1, g1, codes1, scales1)
+        side2 = (x2, g2, codes2, scales2)
+
+        def flip_in(side, c, b, on_vector):
+            x, g = side[0], side[1]
+            xf = x[:].bitcast(F32)
+            gf = g[:].bitcast(F32)
+            tp = ps_ring.tile([P, 512], F32, tag="ring", name="tp")
+            tpv = tp[:].rearrange("p (u r) -> p u r", u=2)
+            for s in range(2):
+                for u in range(2):
+                    nc.tensor.transpose(
+                        tpv[:, u, P * s : P * (s + 1)],
+                        xf[:, TPC * c + 2 * b + s, P * u : P * (u + 1)],
+                        ident[:],
+                    )
+            r0 = CH * c + 256 * b
+            dst = gf[:, r0 : r0 + 256, :]
+            src = tp[:].rearrange("p (u r) -> p r u", u=2)
+            if on_vector:
+                nc.vector.tensor_copy(out=dst, in_=src)
+            else:
+                nc.scalar.copy(out=dst, in_=src)
+
+        def quantise(side, r0, nrows):
+            g, codes, scales = side[1], side[2], side[3]
+            rows = slice(r0, r0 + nrows)
+            nc.vector.quantize_mx(
+                out=codes[:, rows].bitcast(FP8X4),
+                scales=scales[:, rows],
+                in_=g[:, rows, :].rearrange("p r t -> p (r t)"),
+            )
+
+        def square(t):
+            junk = scrap.tile([P, D], BF16, tag="junk")
+            nc.scalar.activation(out=junk[:], in_=x2[:, t, :], func=ACT.Square, accum_out=sq2[:, t : t + 1])
+
+        def halve(t0, t1):
+            nc.scalar.activation(out=half2[:, t0:t1], in_=sq2[:, t0:t1], func=ACT.Copy, scale=0.5)
+
+        fillers = []
+        for x, ntiles, base in ((x1, NT1, 0), (x2, NT2, 4)):
+            for w in range(4):
+                for t in range(ntiles):
+                    fillers.append((x, ntiles, base, w, t))
+        pos = [0]
+
+        def stats1():
+            nc.scalar.activation(out=m1[:], in_=sums[:, 0:4, 0], func=ACT.Copy, scale=1.0 / N1)
+            nc.scalar.activation(out=negm1[:], in_=sums[:, 0:4, 0], func=ACT.Copy, scale=-1.0 / N1)
+            for w in range(4):
+                nc.scalar.activation(
+                    out=junkv[:],
+                    in_=g1[:, :, w],
+                    func=ACT.Square,
+                    bias=negm1[:, w : w + 1],
+                    scale=1.0,
+                    accum_out=dev[:, w : w + 1],
+                )
+
+        def stats2():
+            nc.scalar.activation(out=m2[:], in_=sums[:, 4:8, 0], func=ACT.Copy, scale=1.0 / N2)
+            nc.gpsimd.tensor_tensor(out=diff[:], in0=m1[:], in1=m2[:], op=ALU.subtract)
+            nc.scalar.activation(out=junks[:], in_=diff[:], func=ACT.Square, accum_out=parts[:, 0:1])
+            nc.scalar.activation(
+                out=junks[:], in_=dev[:], func=ACT.Relu, bias=0.1, scale=-1.0 / N1, accum_out=parts[:, 1:2]
+            )
+            nc.scalar.activation(out=junks[:], in_=dev[:], func=ACT.Copy, scale=1.0 / N1, accum_out=parts[:, 2:3])
+            nc.scalar.activation(out=junks[:], in_=m1[:], func=ACT.Square, accum_out=parts[:, 3:4])
+            nc.gpsimd.tensor_tensor(out=sum_a[:], in0=parts[:, 0:1], in1=parts[:, 1:2], op=ALU.add)
+            nc.gpsimd.tensor_tensor(out=sum_b[:], in0=parts[:, 2:3], in1=parts[:, 3:4], op=ALU.add)
+            nc.gpsimd.tensor_scalar(
+                out=rest[:], in0=sum_a[:], scalar1=1.0 / D, scalar2=sum_b[:, 0:1], op0=ALU.mult, op1=ALU.add
+            )
+
+        def fill(n):
+            for rep in range(n):
+                if pos[0] >= len(fillers):
+                    return
+                x, ntiles, base, w, t = fillers[pos[0]]
+                pos[0] += 1
+                nc.tensor.matmul(
+                    out=sums[:, base + w, :],
+                    lhsT=x[:, t, :].rearrange("p (u q e) -> p u e q", u=2, e=2)[:, w // 2, w % 2, :],
+                    rhs=ones[:],
+                    start=(t == 0),
+                    stop=(t == ntiles - 1),
+                )
+                if pos[0] == 4 * NT1:
+                    stats1()
+                if pos[0] == 4 * (NT1 + NT2):
+                    stats2()
+
+        started = set()
+
+        def pair(jt, ib, nfill):
+            ps = ps_ring.tile([P, 512], F32, tag="ring", name="mx")
+            jc = slice(P * jt, P * (jt + 1))
+            ic = slice(512 * ib, 512 * (ib + 1))
+            nc.tensor.matmul_mx(
+                out=ps[:],
+                lhsT=codes2[:, jc].bitcast(FP8X4),
+                lhsT_scale=scales2[:, jc],
+                rhs=codes1[:, ic].bitcast(FP8X4),
+                rhs_scale=scales1[:, ic],
+                start=True,
+                stop=True,
+            )
+            if ib in started:
+                nc.vector.scalar_tensor_tensor(
+                    out=acc[:, ic],
+                    in0=ps[:],
+                    scalar=half2[:, jt : jt + 1],
+                    in1=acc[:, ic],
+                    op0=ALU.subtract,
+                    op1=ALU.max,
+                )
+            else:
+                started.add(ib)
+                nc.vector.tensor_scalar(
+                    out=acc[:, ic],
+                    in0=ps[:],
+                    scalar1=half2[:, jt : jt + 1],
+                    scalar2=None,
+                    op0=ALU.subtract,
+                )
+            fill(nfill)
+
+        flip_in(side1, 0, 0, True)
+        flip_in(side1, 0, 1, False)
+        flip_in(side2, 0, 0, True)
+        square(0)
+        halve(0, 1)
+        square(1)
+        halve(1, 2)
+        quantise(side1, 0, CH)
+        quantise(side2, 0, 256)
+        for ib in range(1, NCH1):
+            flip_in(side1, ib, 0, False)
+            flip_in(side1, ib, 1, False)
+            pair(0, ib - 1, 0)
+            pair(1, ib - 1, 0)
+            quantise(side1, CH * ib, CH)
+        flip_in(side2, 0, 1, False)
+        square(2)
+        square(3)
+        halve(2, 4)
+        pair(0, 3, 0)
+        pair(1, 3, 0)
+        quantise(side2, 256, 256)
+
+        groups = [[(2, 0), (2, 1), (3, 0), (3, 1)], [(2, 2), (2, 3), (3, 2), (3, 3)]]
+        for jt in range(TPC, NT2 - TPC):
+            groups.append([(jt, ib) for ib in range(NCH1)])
+        next_sq = TPC
+        for gi in range(len(groups)):
+            c = gi + 1
+            if c < NCH2:
+                flip_in(side2, c, 0, False)
+                flip_in(side2, c, 1, False)
+            for rep in range(2):
+                if next_sq < NT2:
+                    square(next_sq)
+                    next_sq += 1
+                    if next_sq % TPC == 0:
+                        halve(next_sq - TPC, next_sq)
+            for jt, ib in groups[gi]:
+                pair(jt, ib, 2)
+            if c < NCH2:
+                quantise(side2, CH * c, CH)
+
+        flipped = {}
+
+        def flip_out(ib):
+            ft = ps_ring.tile([P, 512], F32, tag="ring", name="ft")
+            for q in range(4):
+                nc.tensor.transpose(
+                    ft[:, P * q : P * (q + 1)], acc[:, 512 * ib + P * q : 512 * ib + P * (q + 1)], ident[:]
+                )
+            flipped[ib] = ft
+
+        def reduce_block(ib):
+            nc.vector.tensor_reduce(
+                out=best[:, 4 * ib : 4 * (ib + 1)],
+                in_=flipped[ib][:].rearrange("p (c j) -> p c j", c=4),
+                axis=AX.X,
+                op=ALU.max,
+            )
+
+        tail = list(range(NT2 - TPC, NT2))
+        for jt in tail:
+            for ib in (0, 1):
+                pair(jt, ib, 2)
+        flip_out(0)
+        flip_out(1)
+        for jt in tail[:2]:
+            for ib in (2, 3):
+                pair(jt, ib, 2)
+        reduce_block(0)
+        reduce_block(1)
+        for jt in tail[2:]:
+            for ib in (2, 3):
+                pair(jt, ib, 2)
+        flip_out(2)
+        flip_out(3)
+        reduce_block(2)
+        reduce_block(3)
+
+        nc.vector.tensor_reduce(out=total[:], in_=best[:], axis=AX.X, op=ALU.add)
+        nc.vector.scalar_tensor_tensor(
+            out=last[:, 0:1], in0=total[:], scalar=-2.0 / N1, in1=rest[:], op0=ALU.mult, op1=ALU.add
+        )
+        fin = ps_sm.tile([P, P], F32, tag="fin")
+        nc.tensor.transpose(fin[:], last[:], ident[:])
+        nc.vector.tensor_reduce(out=res[:], in_=fin[:], axis=AX.X, op=ALU.add)
+
+        out_view = out
+        for extra in range(2 - out.ndim):
+            out_view = out_view.unsqueeze(0)
+        nc.sync.dma_start(out=out_view, in_=res[0:1, 0:1])

@@ -28,7 +28,8 @@ def tile_customloss_kernel(tc, cluster1, cluster2, out):
     with ExitStack() as ctx:
         keep = ctx.enter_context(tc.tile_pool(name="keep", bufs=1))
         scrap = ctx.enter_context(tc.tile_pool(name="scrap", bufs=2))
-        ps_ring = ctx.enter_context(tc.psum_pool(name="ps_ring", bufs=6))
+        ps_tp = ctx.enter_context(tc.psum_pool(name="ps_tp", bufs=3))
+        ps_mx = ctx.enter_context(tc.psum_pool(name="ps_mx", bufs=4))
         ps_sm = ctx.enter_context(tc.psum_pool(name="ps_sm", bufs=1))
         ctx.enter_context(tc.manual_schedule())
 
@@ -45,7 +46,8 @@ def tile_customloss_kernel(tc, cluster1, cluster2, out):
         ones = keep.tile([P, 2], BF16)
         sq2 = keep.tile([P, NT2], F32)
         half2 = keep.tile([P, NT2], F32)
-        last = keep.tile([P, P], F32)
+        ends = keep.tile([P, 32], F32)
+        weight = keep.tile([P, P], F32)
         m1 = keep.tile([P, 4], F32)
         negm1 = keep.tile([P, 4], F32)
         m2 = keep.tile([P, 4], F32)
@@ -57,27 +59,28 @@ def tile_customloss_kernel(tc, cluster1, cluster2, out):
         sum_a = keep.tile([P, 1], F32)
         sum_b = keep.tile([P, 1], F32)
         rest = keep.tile([P, 1], F32)
-        best = keep.tile([P, NT1], F32)
-        total = keep.tile([P, 1], F32)
         res = keep.tile([P, 1], F32)
         sums = ps_sm.tile([P, 8, 2], F32, tag="sums")
 
         make_identity(nc, ident[:])
         nc.vector.memset(ones[:], 1.0)
-        nc.vector.memset(last[:], 0.0)
+        nc.vector.memset(ends[:], 0.0)
+        nc.vector.memset(weight[:], -2.0 / N1)
 
-        def load(x, src, c):
+        def load(x, src, t0, nt):
             nc.sync.dma_start(
-                out=x[:, TPC * c : TPC * (c + 1), :],
-                in_=src[CH * c : CH * (c + 1), :].rearrange("(p t) k -> p t k", t=TPC),
+                out=x[:, t0 : t0 + nt, :],
+                in_=src[P * t0 : P * (t0 + nt), :].rearrange("(p t) k -> p t k", t=nt),
             )
 
-        load(x1, cluster1, 0)
-        load(x2, cluster2, 0)
+        load(x1, cluster1, 0, 2)
+        load(x1, cluster1, 2, 2)
+        load(x2, cluster2, 0, 2)
         for c in range(1, NCH1):
-            load(x1, cluster1, c)
+            load(x1, cluster1, TPC * c, TPC)
+        load(x2, cluster2, 2, 2)
         for c in range(1, NCH2):
-            load(x2, cluster2, c)
+            load(x2, cluster2, TPC * c, TPC)
 
         side1 = (x1, g1, codes1, scales1)
         side2 = (x2, g2, codes2, scales2)
@@ -86,7 +89,7 @@ def tile_customloss_kernel(tc, cluster1, cluster2, out):
             x, g = side[0], side[1]
             xf = x[:].bitcast(F32)
             gf = g[:].bitcast(F32)
-            tp = ps_ring.tile([P, 512], F32, tag="ring", name="tp")
+            tp = ps_tp.tile([P, 512], F32, tag="tp", name="tp")
             tpv = tp[:].rearrange("p (u r) -> p u r", u=2)
             for s in range(2):
                 for u in range(2):
@@ -153,6 +156,9 @@ def tile_customloss_kernel(tc, cluster1, cluster2, out):
             nc.gpsimd.tensor_scalar(
                 out=rest[:], in0=sum_a[:], scalar1=1.0 / D, scalar2=sum_b[:, 0:1], op0=ALU.mult, op1=ALU.add
             )
+            nc.gpsimd.tensor_scalar(
+                out=ends[:, NT1 : NT1 + 1], in0=rest[:], scalar1=-0.5 * N1, scalar2=0.0, op0=ALU.mult, op1=ALU.add
+            )
 
         def fill(n):
             for rep in range(n):
@@ -174,8 +180,8 @@ def tile_customloss_kernel(tc, cluster1, cluster2, out):
 
         started = set()
 
-        def pair(jt, ib, nfill):
-            ps = ps_ring.tile([P, 512], F32, tag="ring", name="mx")
+        def multiply(jt, ib):
+            ps = ps_mx.tile([P, 512], F32, tag="mx", name="mx")
             jc = slice(P * jt, P * (jt + 1))
             ic = slice(512 * ib, 512 * (ib + 1))
             nc.tensor.matmul_mx(
@@ -187,6 +193,10 @@ def tile_customloss_kernel(tc, cluster1, cluster2, out):
                 start=True,
                 stop=True,
             )
+            return ps
+
+        def fold(ps, jt, ib):
+            ic = slice(512 * ib, 512 * (ib + 1))
             if ib in started:
                 nc.vector.scalar_tensor_tensor(
                     out=acc[:, ic],
@@ -205,33 +215,40 @@ def tile_customloss_kernel(tc, cluster1, cluster2, out):
                     scalar2=None,
                     op0=ALU.subtract,
                 )
+
+        def pair(jt, ib, nfill):
+            fold(multiply(jt, ib), jt, ib)
             fill(nfill)
 
         flip_in(side1, 0, 0, True)
-        flip_in(side1, 0, 1, False)
-        flip_in(side2, 0, 0, True)
+        flip_in(side1, 0, 1, True)
         square(0)
         halve(0, 1)
-        square(1)
-        halve(1, 2)
+        flip_in(side2, 0, 0, False)
         quantise(side1, 0, CH)
         quantise(side2, 0, 256)
-        for ib in range(1, NCH1):
-            flip_in(side1, ib, 0, False)
-            flip_in(side1, ib, 1, False)
-            pair(0, ib - 1, 0)
-            pair(1, ib - 1, 0)
-            quantise(side1, CH * ib, CH)
-        flip_in(side2, 0, 1, False)
-        square(2)
-        square(3)
-        halve(2, 4)
-        pair(0, 3, 0)
-        pair(1, 3, 0)
-        quantise(side2, 256, 256)
+        flip_in(side1, 1, 0, False)
+        flip_in(side1, 1, 1, False)
+        square(1)
+        halve(1, 2)
+        for ib in range(NCH1):
+            pair(0, ib, 0)
+            if ib + 1 < NCH1:
+                quantise(side1, CH * (ib + 1), CH)
+            else:
+                quantise(side2, 256, 256)
+            pair(1, ib, 0)
+            if ib + 2 < NCH1:
+                flip_in(side1, ib + 2, 0, False)
+                flip_in(side1, ib + 2, 1, False)
+            elif ib + 2 == NCH1:
+                flip_in(side2, 0, 1, False)
+                square(2)
+                square(3)
+                halve(2, 4)
 
-        groups = [[(2, 0), (2, 1), (3, 0), (3, 1)], [(2, 2), (2, 3), (3, 2), (3, 3)]]
-        for jt in range(TPC, NT2 - TPC):
+        groups = []
+        for jt in range(2, NT2):
             groups.append([(jt, ib) for ib in range(NCH1)])
         next_sq = TPC
         for gi in range(len(groups)):
@@ -246,14 +263,14 @@ def tile_customloss_kernel(tc, cluster1, cluster2, out):
                     if next_sq % TPC == 0:
                         halve(next_sq - TPC, next_sq)
             for jt, ib in groups[gi]:
-                pair(jt, ib, 2)
+                pair(jt, ib, 0 if c < NCH2 else 3)
             if c < NCH2:
                 quantise(side2, CH * c, CH)
 
         flipped = {}
 
         def flip_out(ib):
-            ft = ps_ring.tile([P, 512], F32, tag="ring", name="ft")
+            ft = ps_tp.tile([P, 512], F32, tag="tp", name="ft")
             for q in range(4):
                 nc.tensor.transpose(
                     ft[:, P * q : P * (q + 1)], acc[:, 512 * ib + P * q : 512 * ib + P * (q + 1)], ident[:]
@@ -262,37 +279,19 @@ def tile_customloss_kernel(tc, cluster1, cluster2, out):
 
         def reduce_block(ib):
             nc.vector.tensor_reduce(
-                out=best[:, 4 * ib : 4 * (ib + 1)],
+                out=ends[:, 4 * ib : 4 * (ib + 1)],
                 in_=flipped[ib][:].rearrange("p (c j) -> p c j", c=4),
                 axis=AX.X,
                 op=ALU.max,
             )
 
-        tail = list(range(NT2 - TPC, NT2))
-        for jt in tail:
-            for ib in (0, 1):
-                pair(jt, ib, 2)
-        flip_out(0)
-        flip_out(1)
-        for jt in tail[:2]:
-            for ib in (2, 3):
-                pair(jt, ib, 2)
-        reduce_block(0)
-        reduce_block(1)
-        for jt in tail[2:]:
-            for ib in (2, 3):
-                pair(jt, ib, 2)
-        flip_out(2)
-        flip_out(3)
-        reduce_block(2)
-        reduce_block(3)
+        for ib in range(NCH1):
+            flip_out(ib)
+        for ib in range(NCH1):
+            reduce_block(ib)
 
-        nc.vector.tensor_reduce(out=total[:], in_=best[:], axis=AX.X, op=ALU.add)
-        nc.vector.scalar_tensor_tensor(
-            out=last[:, 0:1], in0=total[:], scalar=-2.0 / N1, in1=rest[:], op0=ALU.mult, op1=ALU.add
-        )
-        fin = ps_sm.tile([P, P], F32, tag="fin")
-        nc.tensor.transpose(fin[:], last[:], ident[:])
+        fin = ps_tp.tile([P, 32], F32, tag="tp", name="fin")
+        nc.tensor.matmul(out=fin[:], lhsT=weight[:], rhs=ends[:], start=True, stop=True)
         nc.vector.tensor_reduce(out=res[:], in_=fin[:], axis=AX.X, op=ALU.add)
 
         out_view = out

@@ -21,6 +21,11 @@ NCH2 = N2 // CH
 NT1 = N1 // P
 NT2 = N2 // P
 FLOPS = 2 * N1 * N2 * D
+SIDE_AT = {5: 0, 6: 1, 7: 2, 8: 3, 10: 0, 12: 1, 14: 2, 16: 3, 18: 0, 20: 1, 22: 2, 24: 3, 26: 0, 28: 1}
+MERGE_JT = 31
+MERGE_ORDER = (2, 3, 0, 1)
+STATS2_JT = 30
+HUGE = 3.0e38
 
 
 def tile_customloss_kernel(tc, cluster1, cluster2, out):
@@ -28,6 +33,7 @@ def tile_customloss_kernel(tc, cluster1, cluster2, out):
     with ExitStack() as ctx:
         keep = ctx.enter_context(tc.tile_pool(name="keep", bufs=1))
         scrap = ctx.enter_context(tc.tile_pool(name="scrap", bufs=2))
+        side_pool = ctx.enter_context(tc.tile_pool(name="side_pool", bufs=2))
         ps_tp = ctx.enter_context(tc.psum_pool(name="ps_tp", bufs=3))
         ps_mx = ctx.enter_context(tc.psum_pool(name="ps_mx", bufs=4))
         ps_sm = ctx.enter_context(tc.psum_pool(name="ps_sm", bufs=1))
@@ -60,6 +66,11 @@ def tile_customloss_kernel(tc, cluster1, cluster2, out):
         sum_b = keep.tile([P, 1], F32)
         rest = keep.tile([P, 1], F32)
         res = keep.tile([P, 1], F32)
+        fmin = keep.tile([P, NCH1], F32)
+        flo = keep.tile([P, 1], F32)
+        negf = keep.tile([P, 1], F32)
+        negb = keep.tile([P, NT2], F32)
+        acc_y = keep.tile([P, N1], F32)
         sums = ps_sm.tile([P, 8, 2], F32, tag="sums")
 
         make_identity(nc, ident[:])
@@ -129,20 +140,42 @@ def tile_customloss_kernel(tc, cluster1, cluster2, out):
                     fillers.append((x, ntiles, base, w, t))
         pos = [0]
 
+        tasks = []
+        for t in range(TPC, NT2):
+            tasks.append((1, "square", t))
+        tpos = [0]
+
+        def deviation(w):
+            nc.scalar.activation(
+                out=junkv[:],
+                in_=g1[:, :, w],
+                func=ACT.Square,
+                bias=negm1[:, w : w + 1],
+                scale=1.0,
+                accum_out=dev[:, w : w + 1],
+            )
+
+        def scalar_work(budget):
+            left = budget
+            while tpos[0] < len(tasks) and tasks[tpos[0]][0] <= left:
+                weight_of, kind, arg = tasks[tpos[0]]
+                tpos[0] += 1
+                left -= weight_of
+                if kind == "square":
+                    square(arg)
+                    if (arg + 1) % TPC == 0:
+                        halve(arg + 1 - TPC, arg + 1)
+                else:
+                    deviation(arg)
+
         def stats1():
             nc.scalar.activation(out=m1[:], in_=sums[:, 0:4, 0], func=ACT.Copy, scale=1.0 / N1)
             nc.scalar.activation(out=negm1[:], in_=sums[:, 0:4, 0], func=ACT.Copy, scale=-1.0 / N1)
             for w in range(4):
-                nc.scalar.activation(
-                    out=junkv[:],
-                    in_=g1[:, :, w],
-                    func=ACT.Square,
-                    bias=negm1[:, w : w + 1],
-                    scale=1.0,
-                    accum_out=dev[:, w : w + 1],
-                )
+                tasks.append((2, "deviation", w))
 
         def stats2():
+            assert tpos[0] == len(tasks) and pos[0] == len(fillers)
             nc.scalar.activation(out=m2[:], in_=sums[:, 4:8, 0], func=ACT.Copy, scale=1.0 / N2)
             nc.gpsimd.tensor_tensor(out=diff[:], in0=m1[:], in1=m2[:], op=ALU.subtract)
             nc.scalar.activation(out=junks[:], in_=diff[:], func=ACT.Square, accum_out=parts[:, 0:1])
@@ -160,7 +193,12 @@ def tile_customloss_kernel(tc, cluster1, cluster2, out):
                 out=ends[:, NT1 : NT1 + 1], in0=rest[:], scalar1=-0.5 * N1, scalar2=0.0, op0=ALU.mult, op1=ALU.add
             )
 
+        hold = [0]
+
         def fill(n):
+            if hold[0] > 0:
+                hold[0] -= 1
+                return
             for rep in range(n):
                 if pos[0] >= len(fillers):
                     return
@@ -175,8 +213,8 @@ def tile_customloss_kernel(tc, cluster1, cluster2, out):
                 )
                 if pos[0] == 4 * NT1:
                     stats1()
-                if pos[0] == 4 * (NT1 + NT2):
-                    stats2()
+                    hold[0] = 4
+                    return
 
         started = set()
 
@@ -214,7 +252,12 @@ def tile_customloss_kernel(tc, cluster1, cluster2, out):
                     scalar1=half2[:, jt : jt + 1],
                     scalar2=None,
                     op0=ALU.subtract,
+                    op1=ALU.min,
+                    accum_out=fmin[:, ib : ib + 1],
                 )
+
+        def lift(ps, jt, dst):
+            nc.scalar.activation(out=dst, in_=ps[:], func=ACT.Relu, bias=negb[:, jt : jt + 1], scale=1.0)
 
         def pair(jt, ib, nfill):
             fold(multiply(jt, ib), jt, ib)
@@ -247,23 +290,67 @@ def tile_customloss_kernel(tc, cluster1, cluster2, out):
                 square(3)
                 halve(2, 4)
 
-        groups = []
+        nc.vector.tensor_reduce(out=flo[:], in_=fmin[:], axis=AX.X, op=ALU.min)
+        spreads = []
+
+        def merge(ib):
+            ic = slice(512 * ib, 512 * (ib + 1))
+            nc.vector.scalar_tensor_tensor(
+                out=acc[:, ic],
+                in0=acc_y[:, ic],
+                scalar=negf[:, 0:1],
+                in1=acc[:, ic],
+                op0=ALU.subtract,
+                op1=ALU.max,
+            )
+
+        seeded = set()
+        shifted = set()
         for jt in range(2, NT2):
-            groups.append([(jt, ib) for ib in range(NCH1)])
-        next_sq = TPC
-        for gi in range(len(groups)):
-            c = gi + 1
+            c = jt - 1
+            nfill = 0 if c < NCH2 else 3
+            side = SIDE_AT.get(jt, -1)
             if c < NCH2:
                 flip_in(side2, c, 0, False)
                 flip_in(side2, c, 1, False)
-            for rep in range(2):
-                if next_sq < NT2:
-                    square(next_sq)
-                    next_sq += 1
-                    if next_sq % TPC == 0:
-                        halve(next_sq - TPC, next_sq)
-            for jt, ib in groups[gi]:
-                pair(jt, ib, 0 if c < NCH2 else 3)
+            if jt == 3:
+                nc.vector.tensor_reduce(out=negf[:], in_=spreads[0][:], axis=AX.X, op=ALU.max, negate=True)
+            if jt == STATS2_JT:
+                stats2()
+            if jt == MERGE_JT:
+                for ib in MERGE_ORDER:
+                    merge(ib)
+            scalar_work(1 if side >= 0 else 2)
+            if side >= 0 and jt // TPC not in shifted:
+                shifted.add(jt // TPC)
+                cols = slice(TPC * (jt // TPC), TPC * (jt // TPC + 1))
+                nc.scalar.activation(
+                    out=negb[:, cols], in_=half2[:, cols], func=ACT.Identity, bias=negf[:, 0:1], scale=-1.0
+                )
+            for ib in range(NCH1):
+                ic = slice(512 * ib, 512 * (ib + 1))
+                ps = multiply(jt, ib)
+                if ib != side:
+                    fold(ps, jt, ib)
+                elif ib not in seeded:
+                    seeded.add(ib)
+                    lift(ps, jt, acc_y[:, ic])
+                else:
+                    ys = side_pool.tile([P, 512], F32, tag="ys", name="ys")
+                    lift(ps, jt, ys[:])
+                    gain = side_pool.tile([P, 512], F32, tag="gain", name="gain")
+                    nc.gpsimd.tensor_tensor(out=gain[:], in0=ys[:], in1=acc_y[:, ic], op=ALU.subtract)
+                    nc.gpsimd.tensor_scalar(
+                        out=gain[:], in0=gain[:], scalar1=HUGE, scalar2=0.0, op0=ALU.min, op1=ALU.max
+                    )
+                    nc.gpsimd.tensor_tensor(out=acc_y[:, ic], in0=acc_y[:, ic], in1=gain[:], op=ALU.add)
+                fill(nfill)
+            if jt == 2:
+                spread = ps_tp.tile([P, P], F32, tag="tp", name="spread")
+                nc.tensor.matmul(
+                    out=spread[:], lhsT=flo[:, 0:1].to_broadcast([P, P]), rhs=ident[:], start=True, stop=True
+                )
+                spreads.append(spread)
             if c < NCH2:
                 quantise(side2, CH * c, CH)
 

@@ -1,3 +1,4 @@
+import math
 from contextlib import ExitStack
 
 import concourse.mybir as mybir
@@ -21,11 +22,11 @@ NCH2 = N2 // CH
 NT1 = N1 // P
 NT2 = N2 // P
 FLOPS = 2 * N1 * N2 * D
-SIDE_AT = {5: 0, 6: 1, 7: 2, 8: 3, 10: 0, 12: 1, 14: 2, 16: 3, 18: 0, 20: 1, 22: 2, 24: 3, 26: 0, 28: 1}
-MERGE_JT = 31
-MERGE_ORDER = (2, 3, 0, 1)
-STATS2_JT = 30
-HUGE = 3.0e38
+LANE0 = 4
+LANE_ITEMS = 24
+LANE_SLOTS = (6, 78)
+FILL_SLOTS = (8, 84)
+FLIP_SLOTS = {0: 1, 1: 2, 3: 3, 4: 4, 6: 5, 7: 6, 9: 7}
 
 
 def tile_customloss_kernel(tc, cluster1, cluster2, out):
@@ -33,7 +34,7 @@ def tile_customloss_kernel(tc, cluster1, cluster2, out):
     with ExitStack() as ctx:
         keep = ctx.enter_context(tc.tile_pool(name="keep", bufs=1))
         scrap = ctx.enter_context(tc.tile_pool(name="scrap", bufs=2))
-        side_pool = ctx.enter_context(tc.tile_pool(name="side_pool", bufs=2))
+        side_pool = ctx.enter_context(tc.tile_pool(name="side_pool", bufs=4))
         ps_tp = ctx.enter_context(tc.psum_pool(name="ps_tp", bufs=3))
         ps_mx = ctx.enter_context(tc.psum_pool(name="ps_mx", bufs=4))
         ps_sm = ctx.enter_context(tc.psum_pool(name="ps_sm", bufs=1))
@@ -50,28 +51,28 @@ def tile_customloss_kernel(tc, cluster1, cluster2, out):
         acc = keep.tile([P, N1], F32)
         ident = keep.tile([P, P], F32)
         ones = keep.tile([P, 2], BF16)
-        sq2 = keep.tile([P, NT2], F32)
         half2 = keep.tile([P, NT2], F32)
         ends = keep.tile([P, 32], F32)
         weight = keep.tile([P, P], F32)
         m1 = keep.tile([P, 4], F32)
-        negm1 = keep.tile([P, 4], F32)
+        ssq = keep.tile([P, 4], F32)
+        msq = keep.tile([P, 4], F32)
+        m1sq = keep.tile([P, 4], F32)
+        var = keep.tile([P, 4], F32)
         m2 = keep.tile([P, 4], F32)
-        dev = keep.tile([P, 4], F32)
-        junkv = keep.tile([P, N1], BF16)
+        junkv = keep.tile([P, P], F32)
         diff = keep.tile([P, 4], F32)
         parts = keep.tile([P, 4], F32)
         junks = keep.tile([P, 4], F32)
         sum_a = keep.tile([P, 1], F32)
-        sum_b = keep.tile([P, 1], F32)
         rest = keep.tile([P, 1], F32)
         res = keep.tile([P, 1], F32)
+        acc_y = keep.tile([P, N1], F32)
         fmin = keep.tile([P, NCH1], F32)
         flo = keep.tile([P, 1], F32)
         negf = keep.tile([P, 1], F32)
         negb = keep.tile([P, NT2], F32)
-        acc_y = keep.tile([P, N1], F32)
-        sums = ps_sm.tile([P, 8, 2], F32, tag="sums")
+        sums = ps_sm.tile([P, 512], F32, tag="sums")
 
         make_identity(nc, ident[:])
         nc.vector.memset(ones[:], 1.0)
@@ -126,68 +127,56 @@ def tile_customloss_kernel(tc, cluster1, cluster2, out):
                 in_=g[:, rows, :].rearrange("p r t -> p (r t)"),
             )
 
+        ready = set()
+
         def square(t):
             junk = scrap.tile([P, D], BF16, tag="junk")
-            nc.scalar.activation(out=junk[:], in_=x2[:, t, :], func=ACT.Square, accum_out=sq2[:, t : t + 1])
-
-        def halve(t0, t1):
-            nc.scalar.activation(out=half2[:, t0:t1], in_=sq2[:, t0:t1], func=ACT.Copy, scale=0.5)
+            nc.scalar.activation(
+                out=junk[:], in_=x2[:, t, :], func=ACT.Square, scale=math.sqrt(0.5), accum_out=half2[:, t : t + 1]
+            )
+            ready.add(t)
 
         fillers = []
-        for x, ntiles, base in ((x1, NT1, 0), (x2, NT2, 4)):
-            for w in range(4):
-                for t in range(ntiles):
-                    fillers.append((x, ntiles, base, w, t))
+        for w in range(4):
+            for t in range(NT1):
+                fillers.append(("sum", x1, NT1, w, w, t))
+        for w in range(4):
+            for t in range(NT1):
+                fillers.append(("gram", x1, NT1, w, w, t))
+        for w in range(4):
+            for t in range(NT2):
+                fillers.append(("sum", x2, NT2, 4 + w, w, t))
         pos = [0]
 
-        tasks = []
-        for t in range(TPC, NT2):
-            tasks.append((1, "square", t))
-        tpos = [0]
-
-        def deviation(w):
-            nc.scalar.activation(
-                out=junkv[:],
-                in_=g1[:, :, w],
-                func=ACT.Square,
-                bias=negm1[:, w : w + 1],
-                scale=1.0,
-                accum_out=dev[:, w : w + 1],
-            )
-
-        def scalar_work(budget):
-            left = budget
-            while tpos[0] < len(tasks) and tasks[tpos[0]][0] <= left:
-                weight_of, kind, arg = tasks[tpos[0]]
-                tpos[0] += 1
-                left -= weight_of
-                if kind == "square":
-                    square(arg)
-                    if (arg + 1) % TPC == 0:
-                        halve(arg + 1 - TPC, arg + 1)
-                else:
-                    deviation(arg)
-
         def stats1():
-            nc.scalar.activation(out=m1[:], in_=sums[:, 0:4, 0], func=ACT.Copy, scale=1.0 / N1)
-            nc.scalar.activation(out=negm1[:], in_=sums[:, 0:4, 0], func=ACT.Copy, scale=-1.0 / N1)
-            for w in range(4):
-                tasks.append((2, "deviation", w))
+            nc.scalar.activation(out=m1[:], in_=sums[:, 0:8:2], func=ACT.Copy, scale=1.0 / N1)
+
+        def diagonal(w):
+            r = gram_at(w)
+            nc.vector.scalar_tensor_tensor(
+                out=junkv[:],
+                in0=sums[:, r : r + P],
+                scalar=1.0,
+                in1=ident[:],
+                op0=ALU.mult,
+                op1=ALU.mult,
+                accum_out=ssq[:, w : w + 1],
+            )
 
         def stats2():
-            assert tpos[0] == len(tasks) and pos[0] == len(fillers)
-            nc.scalar.activation(out=m2[:], in_=sums[:, 4:8, 0], func=ACT.Copy, scale=1.0 / N2)
+            assert pos[0] == len(fillers)
+            nc.scalar.activation(out=m2[:], in_=sums[:, 8:16:2], func=ACT.Copy, scale=1.0 / N2)
+            nc.scalar.activation(out=msq[:], in_=ssq[:], func=ACT.Copy, scale=1.0 / N1, accum_out=parts[:, 2:3])
+            nc.scalar.activation(out=m1sq[:], in_=m1[:], func=ACT.Square)
             nc.gpsimd.tensor_tensor(out=diff[:], in0=m1[:], in1=m2[:], op=ALU.subtract)
+            nc.gpsimd.tensor_tensor(out=var[:], in0=msq[:], in1=m1sq[:], op=ALU.subtract)
             nc.scalar.activation(out=junks[:], in_=diff[:], func=ACT.Square, accum_out=parts[:, 0:1])
             nc.scalar.activation(
-                out=junks[:], in_=dev[:], func=ACT.Relu, bias=0.1, scale=-1.0 / N1, accum_out=parts[:, 1:2]
+                out=junks[:], in_=var[:], func=ACT.Relu, bias=0.1, scale=-1.0, accum_out=parts[:, 1:2]
             )
-            nc.scalar.activation(out=junks[:], in_=dev[:], func=ACT.Copy, scale=1.0 / N1, accum_out=parts[:, 2:3])
-            nc.scalar.activation(out=junks[:], in_=m1[:], func=ACT.Square, accum_out=parts[:, 3:4])
             nc.gpsimd.tensor_tensor(out=sum_a[:], in0=parts[:, 0:1], in1=parts[:, 1:2], op=ALU.add)
-            nc.gpsimd.tensor_tensor(out=sum_b[:], in0=parts[:, 2:3], in1=parts[:, 3:4], op=ALU.add)
             nc.gpsimd.tensor_scalar(
-                out=rest[:], in0=sum_a[:], scalar1=1.0 / D, scalar2=sum_b[:, 0:1], op0=ALU.mult, op1=ALU.add
+                out=rest[:], in0=sum_a[:], scalar1=1.0 / D, scalar2=parts[:, 2:3], op0=ALU.mult, op1=ALU.add
             )
             nc.gpsimd.tensor_scalar(
                 out=ends[:, NT1 : NT1 + 1], in0=rest[:], scalar1=-0.5 * N1, scalar2=0.0, op0=ALU.mult, op1=ALU.add
@@ -195,31 +184,37 @@ def tile_customloss_kernel(tc, cluster1, cluster2, out):
 
         hold = [0]
 
-        def fill(n):
+        def gram_at(w):
+            return P * (1 + w % 3)
+
+        def fill(target):
             if hold[0] > 0:
                 hold[0] -= 1
                 return
-            for rep in range(n):
-                if pos[0] >= len(fillers):
-                    return
-                x, ntiles, base, w, t = fillers[pos[0]]
+            while pos[0] < min(target, len(fillers)):
+                kind, x, ntiles, place, w, t = fillers[pos[0]]
                 pos[0] += 1
-                nc.tensor.matmul(
-                    out=sums[:, base + w, :],
-                    lhsT=x[:, t, :].rearrange("p (u q e) -> p u e q", u=2, e=2)[:, w // 2, w % 2, :],
-                    rhs=ones[:],
-                    start=(t == 0),
-                    stop=(t == ntiles - 1),
-                )
-                if pos[0] == 4 * NT1:
-                    stats1()
-                    hold[0] = 4
-                    return
+                block = x[:, t, P * w : P * (w + 1)]
+                if kind == "sum":
+                    dst, rhs = sums[:, 2 * place : 2 * place + 2], ones[:]
+                else:
+                    dst, rhs = sums[:, gram_at(w) : gram_at(w) + P], block
+                nc.tensor.matmul(out=dst, lhsT=block, rhs=rhs, start=(t == 0), stop=(t == ntiles - 1))
+                if t == ntiles - 1:
+                    if kind == "sum" and place == 3:
+                        stats1()
+                        hold[0] = 2
+                        return
+                    if kind == "gram" and w >= 2:
+                        for done in (0, 1, 2) if w == 2 else (3,):
+                            diagonal(done)
+                        hold[0] = 2
+                        return
 
         started = set()
 
-        def multiply(jt, ib):
-            ps = ps_mx.tile([P, 512], F32, tag="mx", name="mx")
+        def multiply(jt, ib, pool, tag):
+            ps = pool.tile([P, 512], F32, tag=tag, name="mx")
             jc = slice(P * jt, P * (jt + 1))
             ic = slice(512 * ib, 512 * (ib + 1))
             nc.tensor.matmul_mx(
@@ -234,6 +229,7 @@ def tile_customloss_kernel(tc, cluster1, cluster2, out):
             return ps
 
         def fold(ps, jt, ib):
+            assert jt in ready
             ic = slice(512 * ib, 512 * (ib + 1))
             if ib in started:
                 nc.vector.scalar_tensor_tensor(
@@ -256,31 +252,56 @@ def tile_customloss_kernel(tc, cluster1, cluster2, out):
                     accum_out=fmin[:, ib : ib + 1],
                 )
 
-        def lift(ps, jt, dst):
-            nc.scalar.activation(out=dst, in_=ps[:], func=ACT.Relu, bias=negb[:, jt : jt + 1], scale=1.0)
+        lane = {}
 
-        def pair(jt, ib, nfill):
-            fold(multiply(jt, ib), jt, ib)
-            fill(nfill)
+        def lane_step(k):
+            if k < LANE_ITEMS:
+                jt, ib = LANE0 + k // NCH1, k % NCH1
+                ps = multiply(jt, ib, ps_tp, "tp")
+                if ib == 0:
+                    assert jt in ready
+                    nc.scalar.activation(
+                        out=negb[:, jt : jt + 1],
+                        in_=half2[:, jt : jt + 1],
+                        func=ACT.Identity,
+                        bias=negf[:, 0:1],
+                        scale=-1.0,
+                    )
+                best = acc_y[:, 512 * ib : 512 * (ib + 1)]
+                if k < NCH1:
+                    ys = best
+                else:
+                    ys_tile = side_pool.tile([P, 512], F32, tag="ys", name="ys_tile")
+                    ys = ys_tile[:]
+                nc.scalar.activation(out=ys, in_=ps[:], func=ACT.Relu, bias=negb[:, jt : jt + 1], scale=1.0)
+                lane[k] = (ys, best)
+            if NCH1 <= k - 1 < LANE_ITEMS:
+                ys, best = lane[k - 1]
+                nc.gpsimd.tensor_tensor(out=ys, in0=ys, in1=best, op=ALU.subtract)
+            if NCH1 <= k - 2 < LANE_ITEMS:
+                ys, best = lane[k - 2]
+                nc.scalar.activation(out=ys, in_=ys, func=ACT.Relu)
+                nc.gpsimd.tensor_tensor(out=best, in0=best, in1=ys, op=ALU.add)
+
+        def pair(jt, ib):
+            fold(multiply(jt, ib, ps_mx, "mx"), jt, ib)
 
         flip_in(side1, 0, 0, True)
         flip_in(side1, 0, 1, True)
         square(0)
-        halve(0, 1)
         flip_in(side2, 0, 0, False)
         quantise(side1, 0, CH)
         quantise(side2, 0, 256)
         flip_in(side1, 1, 0, False)
         flip_in(side1, 1, 1, False)
         square(1)
-        halve(1, 2)
         for ib in range(NCH1):
-            pair(0, ib, 0)
+            pair(0, ib)
             if ib + 1 < NCH1:
                 quantise(side1, CH * (ib + 1), CH)
             else:
                 quantise(side2, 256, 256)
-            pair(1, ib, 0)
+            pair(1, ib)
             if ib + 2 < NCH1:
                 flip_in(side1, ib + 2, 0, False)
                 flip_in(side1, ib + 2, 1, False)
@@ -288,10 +309,10 @@ def tile_customloss_kernel(tc, cluster1, cluster2, out):
                 flip_in(side2, 0, 1, False)
                 square(2)
                 square(3)
-                halve(2, 4)
 
         nc.vector.tensor_reduce(out=flo[:], in_=fmin[:], axis=AX.X, op=ALU.min)
-        spreads = []
+        spread = ps_tp.tile([P, P], F32, tag="tp", name="spread")
+        nc.tensor.matmul(out=spread[:], lhsT=flo[:, 0:1].to_broadcast([P, P]), rhs=ident[:], start=True, stop=True)
 
         def merge(ib):
             ic = slice(512 * ib, 512 * (ib + 1))
@@ -304,55 +325,42 @@ def tile_customloss_kernel(tc, cluster1, cluster2, out):
                 op1=ALU.max,
             )
 
-        seeded = set()
-        shifted = set()
-        for jt in range(2, NT2):
-            c = jt - 1
-            nfill = 0 if c < NCH2 else 3
-            side = SIDE_AT.get(jt, -1)
-            if c < NCH2:
-                flip_in(side2, c, 0, False)
-                flip_in(side2, c, 1, False)
-            if jt == 3:
-                nc.vector.tensor_reduce(out=negf[:], in_=spreads[0][:], axis=AX.X, op=ALU.max, negate=True)
-            if jt == STATS2_JT:
-                stats2()
-            if jt == MERGE_JT:
-                for ib in MERGE_ORDER:
-                    merge(ib)
-            scalar_work(1 if side >= 0 else 2)
-            if side >= 0 and jt // TPC not in shifted:
-                shifted.add(jt // TPC)
-                cols = slice(TPC * (jt // TPC), TPC * (jt // TPC + 1))
-                nc.scalar.activation(
-                    out=negb[:, cols], in_=half2[:, cols], func=ACT.Identity, bias=negf[:, 0:1], scale=-1.0
-                )
-            for ib in range(NCH1):
-                ic = slice(512 * ib, 512 * (ib + 1))
-                ps = multiply(jt, ib)
-                if ib != side:
-                    fold(ps, jt, ib)
-                elif ib not in seeded:
-                    seeded.add(ib)
-                    lift(ps, jt, acc_y[:, ic])
-                else:
-                    ys = side_pool.tile([P, 512], F32, tag="ys", name="ys")
-                    lift(ps, jt, ys[:])
-                    gain = side_pool.tile([P, 512], F32, tag="gain", name="gain")
-                    nc.gpsimd.tensor_tensor(out=gain[:], in0=ys[:], in1=acc_y[:, ic], op=ALU.subtract)
-                    nc.gpsimd.tensor_scalar(
-                        out=gain[:], in0=gain[:], scalar1=HUGE, scalar2=0.0, op0=ALU.min, op1=ALU.max
-                    )
-                    nc.gpsimd.tensor_tensor(out=acc_y[:, ic], in0=acc_y[:, ic], in1=gain[:], op=ALU.add)
-                fill(nfill)
-            if jt == 2:
-                spread = ps_tp.tile([P, P], F32, tag="tp", name="spread")
-                nc.tensor.matmul(
-                    out=spread[:], lhsT=flo[:, 0:1].to_broadcast([P, P]), rhs=ident[:], start=True, stop=True
-                )
-                spreads.append(spread)
-            if c < NCH2:
-                quantise(side2, CH * c, CH)
+        in_lane = {(LANE0 + k // NCH1, k % NCH1) for k in range(LANE_ITEMS)}
+        slots = [(jt, ib) for jt in range(2, NT2 - 2) for ib in range(NCH1) if (jt, ib) not in in_lane]
+        n_steps = LANE_ITEMS + 2
+        step_slot = [LANE_SLOTS[0] + k * (LANE_SLOTS[1] - LANE_SLOTS[0]) // n_steps for k in range(n_steps)]
+        need = {}
+        for s in range(len(slots)):
+            need.setdefault(slots[s][0], s - 6)
+        for k in range(0, LANE_ITEMS, NCH1):
+            need[LANE0 + k // NCH1] = min(need.get(LANE0 + k // NCH1, 999), step_slot[k] - 5)
+        need[NT2 - 2] = len(slots) - 6
+        need[NT2 - 1] = len(slots) - 4
+        squares = sorted([(need[t], t) for t in range(TPC, NT2)])
+        steps = [0]
+        waiting = []
+        for s in range(len(slots)):
+            jt, ib = slots[s]
+            if s in FLIP_SLOTS:
+                flip_in(side2, FLIP_SLOTS[s], 0, False)
+                flip_in(side2, FLIP_SLOTS[s], 1, False)
+                waiting.append((s + 3, FLIP_SLOTS[s]))
+            while squares and squares[0][0] <= s:
+                square(squares.pop(0)[1])
+            pair(jt, ib)
+            if s == 0:
+                nc.vector.tensor_reduce(out=negf[:], in_=spread[:], axis=AX.X, op=ALU.max, negate=True)
+            fill(len(fillers) * (s - FILL_SLOTS[0]) // (FILL_SLOTS[1] - FILL_SLOTS[0]))
+            while steps[0] < n_steps and step_slot[steps[0]] <= s:
+                lane_step(steps[0])
+                steps[0] += 1
+            while waiting and waiting[0][0] <= s:
+                quantise(side2, CH * waiting.pop(0)[1], CH)
+        while steps[0] < n_steps:
+            lane_step(steps[0])
+            steps[0] += 1
+        fill(len(fillers))
+        stats2()
 
         flipped = {}
 
@@ -372,9 +380,26 @@ def tile_customloss_kernel(tc, cluster1, cluster2, out):
                 op=ALU.max,
             )
 
-        for ib in range(NCH1):
+        last = [(jt, ib) for b in (0, 2) for jt in (NT2 - 2, NT2 - 1) for ib in (b, b + 1)]
+        banks = [multiply(jt, ib, ps_mx, "mx") for jt, ib in last[0:4]]
+        for i in range(8):
+            jt, ib = last[i]
+            fold(banks[i], jt, ib)
+            if i + 4 < 8:
+                banks.append(multiply(last[i + 4][0], last[i + 4][1], ps_mx, "mx"))
+            if i == 1:
+                merge(0)
+                merge(1)
+            if i == 3:
+                flip_out(0)
+                flip_out(1)
+                merge(2)
+                merge(3)
+            if i == 5:
+                reduce_block(0)
+        reduce_block(1)
+        for ib in (2, 3):
             flip_out(ib)
-        for ib in range(NCH1):
             reduce_block(ib)
 
         fin = ps_tp.tile([P, 32], F32, tag="tp", name="fin")

@@ -23,10 +23,12 @@ NT1 = N1 // P
 NT2 = N2 // P
 FLOPS = 2 * N1 * N2 * D
 LANE0 = 4
-LANE_ITEMS = 24
-LANE_SLOTS = (6, 78)
-FILL_SLOTS = (8, 84)
-FLIP_SLOTS = {0: 1, 1: 2, 3: 3, 4: 4, 6: 5, 7: 6, 9: 7}
+LANE_ITEMS = 20
+LANE_START = 6
+LANE_ROW = 19
+FILL_SLOTS = (13, 89)
+DEVIATION_SLOTS = (41, 85)
+FLIP_CHUNK0 = 2
 
 
 def tile_customloss_kernel(tc, cluster1, cluster2, out):
@@ -34,7 +36,7 @@ def tile_customloss_kernel(tc, cluster1, cluster2, out):
     with ExitStack() as ctx:
         keep = ctx.enter_context(tc.tile_pool(name="keep", bufs=1))
         scrap = ctx.enter_context(tc.tile_pool(name="scrap", bufs=2))
-        side_pool = ctx.enter_context(tc.tile_pool(name="side_pool", bufs=4))
+        side_pool = ctx.enter_context(tc.tile_pool(name="side_pool", bufs=2))
         ps_tp = ctx.enter_context(tc.psum_pool(name="ps_tp", bufs=3))
         ps_mx = ctx.enter_context(tc.psum_pool(name="ps_mx", bufs=4))
         ps_sm = ctx.enter_context(tc.psum_pool(name="ps_sm", bufs=1))
@@ -55,12 +57,12 @@ def tile_customloss_kernel(tc, cluster1, cluster2, out):
         ends = keep.tile([P, 32], F32)
         weight = keep.tile([P, P], F32)
         m1 = keep.tile([P, 4], F32)
-        ssq = keep.tile([P, 4], F32)
-        msq = keep.tile([P, 4], F32)
-        m1sq = keep.tile([P, 4], F32)
+        negm1 = keep.tile([P, 4], F32)
+        dev = keep.tile([P, 2, 4], F32)
+        junkd = keep.tile([P, 1024], BF16)
+        sum_b = keep.tile([P, 1], F32)
         var = keep.tile([P, 4], F32)
         m2 = keep.tile([P, 4], F32)
-        junkv = keep.tile([P, P], F32)
         diff = keep.tile([P, 4], F32)
         parts = keep.tile([P, 4], F32)
         junks = keep.tile([P, 4], F32)
@@ -72,7 +74,6 @@ def tile_customloss_kernel(tc, cluster1, cluster2, out):
         flo = keep.tile([P, 1], F32)
         negf = keep.tile([P, 1], F32)
         negb = keep.tile([P, NT2], F32)
-        sums = ps_sm.tile([P, 512], F32, tag="sums")
 
         make_identity(nc, ident[:])
         nc.vector.memset(ones[:], 1.0)
@@ -137,46 +138,44 @@ def tile_customloss_kernel(tc, cluster1, cluster2, out):
             ready.add(t)
 
         fillers = []
-        for w in range(4):
-            for t in range(NT1):
-                fillers.append(("sum", x1, NT1, w, w, t))
-        for w in range(4):
-            for t in range(NT1):
-                fillers.append(("gram", x1, NT1, w, w, t))
-        for w in range(4):
-            for t in range(NT2):
-                fillers.append(("sum", x2, NT2, 4 + w, w, t))
+        for kind, x, ntiles in (("sum1", x1, NT1), ("sum2", x2, NT2)):
+            for w in range(4):
+                for t in range(ntiles):
+                    fillers.append((kind, x, ntiles, w, t))
         pos = [0]
+        bank = {}
 
-        def stats1():
-            nc.scalar.activation(out=m1[:], in_=sums[:, 0:8:2], func=ACT.Copy, scale=1.0 / N1)
+        def finish(kind):
+            if kind == "sum1":
+                nc.scalar.activation(out=m1[:], in_=bank[kind][:, 0:8:2], func=ACT.Copy, scale=1.0 / N1)
+                nc.scalar.activation(out=negm1[:], in_=bank[kind][:, 0:8:2], func=ACT.Copy, scale=-1.0 / N1)
+            else:
+                nc.scalar.activation(out=m2[:], in_=bank[kind][:, 0:8:2], func=ACT.Copy, scale=1.0 / N2)
 
-        def diagonal(w):
-            r = gram_at(w)
-            nc.vector.scalar_tensor_tensor(
-                out=junkv[:],
-                in0=sums[:, r : r + P],
-                scalar=1.0,
-                in1=ident[:],
-                op0=ALU.mult,
-                op1=ALU.mult,
-                accum_out=ssq[:, w : w + 1],
+        def deviation(w, h):
+            nc.scalar.activation(
+                out=junkd[:],
+                in_=g1[:, 1024 * h : 1024 * (h + 1), w],
+                func=ACT.Square,
+                bias=negm1[:, w : w + 1],
+                scale=1.0,
+                accum_out=dev[:, h, w : w + 1],
             )
 
         def stats2():
             assert pos[0] == len(fillers)
-            nc.scalar.activation(out=m2[:], in_=sums[:, 8:16:2], func=ACT.Copy, scale=1.0 / N2)
-            nc.scalar.activation(out=msq[:], in_=ssq[:], func=ACT.Copy, scale=1.0 / N1, accum_out=parts[:, 2:3])
-            nc.scalar.activation(out=m1sq[:], in_=m1[:], func=ACT.Square)
             nc.gpsimd.tensor_tensor(out=diff[:], in0=m1[:], in1=m2[:], op=ALU.subtract)
-            nc.gpsimd.tensor_tensor(out=var[:], in0=msq[:], in1=m1sq[:], op=ALU.subtract)
+            nc.gpsimd.tensor_tensor(out=var[:], in0=dev[:, 0, :], in1=dev[:, 1, :], op=ALU.add)
+            nc.scalar.activation(out=junks[:], in_=var[:], func=ACT.Copy, scale=1.0 / N1, accum_out=parts[:, 2:3])
+            nc.scalar.activation(out=junks[:], in_=m1[:], func=ACT.Square, accum_out=parts[:, 3:4])
             nc.scalar.activation(out=junks[:], in_=diff[:], func=ACT.Square, accum_out=parts[:, 0:1])
             nc.scalar.activation(
-                out=junks[:], in_=var[:], func=ACT.Relu, bias=0.1, scale=-1.0, accum_out=parts[:, 1:2]
+                out=junks[:], in_=var[:], func=ACT.Relu, bias=0.1, scale=-1.0 / N1, accum_out=parts[:, 1:2]
             )
             nc.gpsimd.tensor_tensor(out=sum_a[:], in0=parts[:, 0:1], in1=parts[:, 1:2], op=ALU.add)
+            nc.gpsimd.tensor_tensor(out=sum_b[:], in0=parts[:, 2:3], in1=parts[:, 3:4], op=ALU.add)
             nc.gpsimd.tensor_scalar(
-                out=rest[:], in0=sum_a[:], scalar1=1.0 / D, scalar2=parts[:, 2:3], op0=ALU.mult, op1=ALU.add
+                out=rest[:], in0=sum_a[:], scalar1=1.0 / D, scalar2=sum_b[:, 0:1], op0=ALU.mult, op1=ALU.add
             )
             nc.gpsimd.tensor_scalar(
                 out=ends[:, NT1 : NT1 + 1], in0=rest[:], scalar1=-0.5 * N1, scalar2=0.0, op0=ALU.mult, op1=ALU.add
@@ -184,32 +183,22 @@ def tile_customloss_kernel(tc, cluster1, cluster2, out):
 
         hold = [0]
 
-        def gram_at(w):
-            return P * (1 + w % 3)
-
         def fill(target):
             if hold[0] > 0:
                 hold[0] -= 1
                 return
             while pos[0] < min(target, len(fillers)):
-                kind, x, ntiles, place, w, t = fillers[pos[0]]
+                kind, x, ntiles, w, t = fillers[pos[0]]
                 pos[0] += 1
-                block = x[:, t, P * w : P * (w + 1)]
-                if kind == "sum":
-                    dst, rhs = sums[:, 2 * place : 2 * place + 2], ones[:]
-                else:
-                    dst, rhs = sums[:, gram_at(w) : gram_at(w) + P], block
-                nc.tensor.matmul(out=dst, lhsT=block, rhs=rhs, start=(t == 0), stop=(t == ntiles - 1))
-                if t == ntiles - 1:
-                    if kind == "sum" and place == 3:
-                        stats1()
-                        hold[0] = 2
-                        return
-                    if kind == "gram" and w >= 2:
-                        for done in (0, 1, 2) if w == 2 else (3,):
-                            diagonal(done)
-                        hold[0] = 2
-                        return
+                if w == 0 and t == 0:
+                    bank[kind] = ps_sm.tile([P, 512], F32, tag="sums", name="sums")
+                block = x[:, t, :].rearrange("p (u q e) -> p u e q", u=2, e=2)[:, w // 2, w % 2, :]
+                dst = bank[kind][:, 2 * w : 2 * w + 2]
+                nc.tensor.matmul(out=dst, lhsT=block, rhs=ones[:], start=(t == 0), stop=(t == ntiles - 1))
+                if w == 3 and t == ntiles - 1:
+                    finish(kind)
+                    hold[0] = 2
+                    return
 
         started = set()
 
@@ -254,65 +243,80 @@ def tile_customloss_kernel(tc, cluster1, cluster2, out):
 
         lane = {}
 
-        def lane_step(k):
-            if k < LANE_ITEMS:
-                jt, ib = LANE0 + k // NCH1, k % NCH1
-                ps = multiply(jt, ib, ps_tp, "tp")
-                if ib == 0:
-                    assert jt in ready
-                    nc.scalar.activation(
-                        out=negb[:, jt : jt + 1],
-                        in_=half2[:, jt : jt + 1],
-                        func=ACT.Identity,
-                        bias=negf[:, 0:1],
-                        scale=-1.0,
-                    )
-                best = acc_y[:, 512 * ib : 512 * (ib + 1)]
-                if k < NCH1:
-                    ys = best
-                else:
-                    ys_tile = side_pool.tile([P, 512], F32, tag="ys", name="ys_tile")
-                    ys = ys_tile[:]
-                nc.scalar.activation(out=ys, in_=ps[:], func=ACT.Relu, bias=negb[:, jt : jt + 1], scale=1.0)
-                lane[k] = (ys, best)
-            if NCH1 <= k - 1 < LANE_ITEMS:
-                ys, best = lane[k - 1]
-                nc.gpsimd.tensor_tensor(out=ys, in0=ys, in1=best, op=ALU.subtract)
-            if NCH1 <= k - 2 < LANE_ITEMS:
-                ys, best = lane[k - 2]
-                nc.scalar.activation(out=ys, in_=ys, func=ACT.Relu)
-                nc.gpsimd.tensor_tensor(out=best, in0=best, in1=ys, op=ALU.add)
+        def lift(k):
+            jt, ib = LANE0 + k // NCH1, k % NCH1
+            assert jt in ready
+            ps = multiply(jt, ib, ps_tp, "tp")
+            if ib == 0:
+                nc.scalar.activation(
+                    out=negb[:, jt : jt + 1],
+                    in_=half2[:, jt : jt + 1],
+                    func=ACT.Identity,
+                    bias=negf[:, 0:1],
+                    scale=-1.0,
+                )
+            n, h = k // NCH1, ib // 2
+            if n == 0:
+                dst = acc_y[:, 512 * ib : 512 * (ib + 1)]
+            else:
+                if ib % 2 == 0:
+                    lane[n, h] = side_pool.tile([P, 1024], F32, tag="ys%d" % h, name="ys")
+                dst = lane[n, h][:, 512 * (ib % 2) : 512 * (ib % 2 + 1)]
+            nc.scalar.activation(out=dst, in_=ps[:], func=ACT.Relu, bias=negb[:, jt : jt + 1], scale=1.0)
+
+        def gain(n, h):
+            ys = lane[n, h]
+            nc.gpsimd.tensor_tensor(
+                out=ys[:], in0=ys[:], in1=acc_y[:, 1024 * h : 1024 * (h + 1)], op=ALU.subtract
+            )
+
+        def raise_maximum(n, h):
+            ys = lane[n, h]
+            best = acc_y[:, 1024 * h : 1024 * (h + 1)]
+            nc.scalar.activation(out=ys[:], in_=ys[:], func=ACT.Relu)
+            nc.gpsimd.tensor_tensor(out=best, in0=best, in1=ys[:], op=ALU.add)
 
         def pair(jt, ib):
             fold(multiply(jt, ib, ps_mx, "mx"), jt, ib)
 
         flip_in(side1, 0, 0, True)
-        flip_in(side1, 0, 1, True)
-        square(0)
+        flip_in(side1, 0, 1, False)
         flip_in(side2, 0, 0, False)
         quantise(side1, 0, CH)
         quantise(side2, 0, 256)
         flip_in(side1, 1, 0, False)
         flip_in(side1, 1, 1, False)
+        square(0)
+        pair(0, 0)
+        flip_in(side1, 2, 0, False)
+        flip_in(side1, 2, 1, False)
+        quantise(side1, CH, CH)
         square(1)
-        for ib in range(NCH1):
-            pair(0, ib)
-            if ib + 1 < NCH1:
-                quantise(side1, CH * (ib + 1), CH)
-            else:
-                quantise(side2, 256, 256)
-            pair(1, ib)
-            if ib + 2 < NCH1:
-                flip_in(side1, ib + 2, 0, False)
-                flip_in(side1, ib + 2, 1, False)
-            elif ib + 2 == NCH1:
-                flip_in(side2, 0, 1, False)
-                square(2)
-                square(3)
-
+        flip_in(side1, 3, 0, False)
+        flip_in(side1, 3, 1, False)
+        pair(1, 0)
+        pair(0, 1)
+        quantise(side1, 2 * CH, CH)
+        flip_in(side2, 0, 1, False)
+        pair(1, 1)
+        flip_in(side2, 1, 0, False)
+        pair(0, 2)
+        quantise(side1, 3 * CH, CH)
+        flip_in(side2, 1, 1, False)
+        pair(1, 2)
+        pair(0, 3)
+        quantise(side2, 256, 256)
+        square(2)
+        pair(1, 3)
         nc.vector.tensor_reduce(out=flo[:], in_=fmin[:], axis=AX.X, op=ALU.min)
-        spread = ps_tp.tile([P, P], F32, tag="tp", name="spread")
-        nc.tensor.matmul(out=spread[:], lhsT=flo[:, 0:1].to_broadcast([P, P]), rhs=ident[:], start=True, stop=True)
+        quantise(side2, CH, CH)
+
+        def find_floor():
+            spread = ps_sm.tile([P, 512], F32, tag="sums", name="spread")
+            nc.tensor.matmul(
+                out=spread[:, 0:P], lhsT=flo[:, 0:1].to_broadcast([P, P]), rhs=ident[:], start=True, stop=True
+            )
+            return spread
 
         def merge(ib):
             ic = slice(512 * ib, 512 * (ib + 1))
@@ -327,38 +331,59 @@ def tile_customloss_kernel(tc, cluster1, cluster2, out):
 
         in_lane = {(LANE0 + k // NCH1, k % NCH1) for k in range(LANE_ITEMS)}
         slots = [(jt, ib) for jt in range(2, NT2 - 2) for ib in range(NCH1) if (jt, ib) not in in_lane]
-        n_steps = LANE_ITEMS + 2
-        step_slot = [LANE_SLOTS[0] + k * (LANE_SLOTS[1] - LANE_SLOTS[0]) // n_steps for k in range(n_steps)]
+        events = {}
+
+        def at(slot, what, *args):
+            events.setdefault(slot, []).append((what, args))
+
+        first_row = LANE_START + 4
+        for i in range(8):
+            n, h = (i // 2) % 2, i // 4
+            at(LANE_START + i, lift, NCH1 * n + 2 * h + i % 2)
+        n_rows = (LANE_ITEMS - 1) // NCH1
+        for n in range(1, n_rows + 1):
+            base = first_row + LANE_ROW * (n - 1)
+            for h in range(2):
+                if NCH1 * n + 2 * h < LANE_ITEMS:
+                    at(base + LANE_ROW * h // 4, gain, n, h)
+                    at(base + LANE_ROW * (4 + 3 * h) // 12, raise_maximum, n, h)
+            for i in range(4):
+                if NCH1 * (n + 1) + i < LANE_ITEMS:
+                    at(base + LANE_ROW * (i + 1) // 5, lift, NCH1 * (n + 1) + i)
+        for i in range(8):
+            at(DEVIATION_SLOTS[0] + i * (DEVIATION_SLOTS[1] - DEVIATION_SLOTS[0]) // 8, deviation, i // 2, i % 2)
         need = {}
         for s in range(len(slots)):
-            need.setdefault(slots[s][0], s - 6)
-        for k in range(0, LANE_ITEMS, NCH1):
-            need[LANE0 + k // NCH1] = min(need.get(LANE0 + k // NCH1, 999), step_slot[k] - 5)
+            need.setdefault(slots[s][0], max(s - 5, 0))
+        for slot in events:
+            for what, args in events[slot]:
+                if what is lift and args[0] % NCH1 == 0:
+                    jt = LANE0 + args[0] // NCH1
+                    need[jt] = min(need.get(jt, 999), slot - 1)
         need[NT2 - 2] = len(slots) - 6
         need[NT2 - 1] = len(slots) - 4
-        squares = sorted([(need[t], t) for t in range(TPC, NT2)])
-        steps = [0]
-        waiting = []
+        for c in range(FLIP_CHUNK0, NCH2):
+            at(c, quantise, side2, CH * c, CH)
+        squares = sorted([(need[t], t) for t in need if t not in ready])
+        spread = None
         for s in range(len(slots)):
             jt, ib = slots[s]
-            if s in FLIP_SLOTS:
-                flip_in(side2, FLIP_SLOTS[s], 0, False)
-                flip_in(side2, FLIP_SLOTS[s], 1, False)
-                waiting.append((s + 3, FLIP_SLOTS[s]))
+            if FLIP_CHUNK0 + s < NCH2:
+                flip_in(side2, FLIP_CHUNK0 + s, 0, False)
+                flip_in(side2, FLIP_CHUNK0 + s, 1, False)
             while squares and squares[0][0] <= s:
                 square(squares.pop(0)[1])
             pair(jt, ib)
-            if s == 0:
-                nc.vector.tensor_reduce(out=negf[:], in_=spread[:], axis=AX.X, op=ALU.max, negate=True)
+            if s == 1:
+                spread = find_floor()
+            if s == 3:
+                nc.vector.tensor_reduce(out=negf[:], in_=spread[:, 0:P], axis=AX.X, op=ALU.max, negate=True)
             fill(len(fillers) * (s - FILL_SLOTS[0]) // (FILL_SLOTS[1] - FILL_SLOTS[0]))
-            while steps[0] < n_steps and step_slot[steps[0]] <= s:
-                lane_step(steps[0])
-                steps[0] += 1
-            while waiting and waiting[0][0] <= s:
-                quantise(side2, CH * waiting.pop(0)[1], CH)
-        while steps[0] < n_steps:
-            lane_step(steps[0])
-            steps[0] += 1
+            for what, args in events.get(s, ()):
+                what(*args)
+            if s >= len(slots) - 4 and s % 2 == 0:
+                merge((s - len(slots) + 4) // 2)
+        assert not squares
         fill(len(fillers))
         stats2()
 
@@ -380,7 +405,7 @@ def tile_customloss_kernel(tc, cluster1, cluster2, out):
                 op=ALU.max,
             )
 
-        last = [(jt, ib) for b in (0, 2) for jt in (NT2 - 2, NT2 - 1) for ib in (b, b + 1)]
+        last = [(jt, ib) for b in (2, 0) for jt in (NT2 - 2, NT2 - 1) for ib in (b, b + 1)]
         banks = [multiply(jt, ib, ps_mx, "mx") for jt, ib in last[0:4]]
         for i in range(8):
             jt, ib = last[i]
@@ -388,18 +413,17 @@ def tile_customloss_kernel(tc, cluster1, cluster2, out):
             if i + 4 < 8:
                 banks.append(multiply(last[i + 4][0], last[i + 4][1], ps_mx, "mx"))
             if i == 1:
-                merge(0)
-                merge(1)
-            if i == 3:
-                flip_out(0)
-                flip_out(1)
                 merge(2)
                 merge(3)
+            if i == 3:
+                flip_out(2)
+                flip_out(3)
             if i == 5:
-                reduce_block(0)
-        reduce_block(1)
-        for ib in (2, 3):
-            flip_out(ib)
+                reduce_block(2)
+            if i == 6:
+                flip_out(0)
+        flip_out(1)
+        for ib in (3, 0, 1):
             reduce_block(ib)
 
         fin = ps_tp.tile([P, 32], F32, tag="tp", name="fin")

@@ -24,11 +24,16 @@ NT2 = N2 // P
 FLOPS = 2 * N1 * N2 * D
 LANE0 = 4
 LANE_ITEMS = 20
-LANE_START = 6
-LANE_ROW = 19
+SQ_MARGIN = 10
+SQ_FROM = 12
+RELU_AT = 4
+LIFT_AT = 2
+LANE_START = 12
+LANE_ROW = 18
 FILL_SLOTS = (13, 89)
 DEVIATION_SLOTS = (41, 85)
-FLIP_CHUNK0 = 2
+WARM = (5, 1, 1, 1, 1, 1)
+FLIP_EVERY = 4
 
 
 def tile_customloss_kernel(tc, cluster1, cluster2, out):
@@ -279,34 +284,49 @@ def tile_customloss_kernel(tc, cluster1, cluster2, out):
         def pair(jt, ib):
             fold(multiply(jt, ib, ps_mx, "mx"), jt, ib)
 
+        warm = keep.tile([P, 512], BF16)
+        nc.vector.memset(warm[:], 0.0)
+        idle = ps_sm.tile([P, 512], F32, tag="sums", name="idle")
+
+        def keep_warm(n):
+            for rep in range(n):
+                nc.tensor.matmul(out=idle[:], lhsT=warm[:, 0:P], rhs=warm[:], start=True, stop=True)
+
+        keep_warm(WARM[0])
         flip_in(side1, 0, 0, True)
-        flip_in(side1, 0, 1, False)
+        keep_warm(WARM[1])
+        flip_in(side1, 0, 1, True)
+        keep_warm(WARM[2])
         flip_in(side2, 0, 0, False)
+        keep_warm(WARM[3])
         quantise(side1, 0, CH)
         quantise(side2, 0, 256)
-        flip_in(side1, 1, 0, False)
-        flip_in(side1, 1, 1, False)
         square(0)
+        flip_in(side1, 1, 0, True)
+        flip_in(side1, 1, 1, False)
+        keep_warm(WARM[4])
         pair(0, 0)
-        flip_in(side1, 2, 0, False)
-        flip_in(side1, 2, 1, False)
         quantise(side1, CH, CH)
         square(1)
+        flip_in(side1, 2, 0, False)
+        flip_in(side1, 2, 1, False)
+        keep_warm(WARM[5])
+        pair(1, 0)
+        quantise(side1, 2 * CH, CH)
+        pair(0, 1)
         flip_in(side1, 3, 0, False)
         flip_in(side1, 3, 1, False)
-        pair(1, 0)
-        pair(0, 1)
-        quantise(side1, 2 * CH, CH)
-        flip_in(side2, 0, 1, False)
         pair(1, 1)
-        flip_in(side2, 1, 0, False)
-        pair(0, 2)
         quantise(side1, 3 * CH, CH)
-        flip_in(side2, 1, 1, False)
+        flip_in(side2, 0, 1, False)
+        pair(0, 2)
+        flip_in(side2, 1, 0, False)
         pair(1, 2)
-        pair(0, 3)
         quantise(side2, 256, 256)
+        pair(0, 3)
+        flip_in(side2, 1, 1, False)
         square(2)
+        square(3)
         pair(1, 3)
         nc.vector.tensor_reduce(out=flo[:], in_=fmin[:], axis=AX.X, op=ALU.min)
         quantise(side2, CH, CH)
@@ -346,15 +366,15 @@ def tile_customloss_kernel(tc, cluster1, cluster2, out):
             for h in range(2):
                 if NCH1 * n + 2 * h < LANE_ITEMS:
                     at(base + LANE_ROW * h // 4, gain, n, h)
-                    at(base + LANE_ROW * (4 + 3 * h) // 12, raise_maximum, n, h)
+                    at(base + LANE_ROW * (RELU_AT + 3 * h) // 12, raise_maximum, n, h)
             for i in range(4):
                 if NCH1 * (n + 1) + i < LANE_ITEMS:
-                    at(base + LANE_ROW * (i + 1) // 5, lift, NCH1 * (n + 1) + i)
+                    at(base + LANE_ROW * (2 * i + LIFT_AT) // 8, lift, NCH1 * (n + 1) + i)
         for i in range(8):
             at(DEVIATION_SLOTS[0] + i * (DEVIATION_SLOTS[1] - DEVIATION_SLOTS[0]) // 8, deviation, i // 2, i % 2)
         need = {}
         for s in range(len(slots)):
-            need.setdefault(slots[s][0], max(s - 5, 0))
+            need.setdefault(slots[s][0], max(s - SQ_MARGIN, min(s - 5, SQ_FROM), 0))
         for slot in events:
             for what, args in events[slot]:
                 if what is lift and args[0] % NCH1 == 0:
@@ -362,15 +382,16 @@ def tile_customloss_kernel(tc, cluster1, cluster2, out):
                     need[jt] = min(need.get(jt, 999), slot - 1)
         need[NT2 - 2] = len(slots) - 6
         need[NT2 - 1] = len(slots) - 4
-        for c in range(FLIP_CHUNK0, NCH2):
-            at(c, quantise, side2, CH * c, CH)
+        flips = {FLIP_EVERY * (c - 2) // 2: c for c in range(2, NCH2)}
+        for s in flips:
+            at(s + 3, quantise, side2, CH * flips[s], CH)
         squares = sorted([(need[t], t) for t in need if t not in ready])
         spread = None
         for s in range(len(slots)):
             jt, ib = slots[s]
-            if FLIP_CHUNK0 + s < NCH2:
-                flip_in(side2, FLIP_CHUNK0 + s, 0, False)
-                flip_in(side2, FLIP_CHUNK0 + s, 1, False)
+            if s in flips:
+                flip_in(side2, flips[s], 0, False)
+                flip_in(side2, flips[s], 1, False)
             while squares and squares[0][0] <= s:
                 square(squares.pop(0)[1])
             pair(jt, ib)
@@ -381,8 +402,6 @@ def tile_customloss_kernel(tc, cluster1, cluster2, out):
             fill(len(fillers) * (s - FILL_SLOTS[0]) // (FILL_SLOTS[1] - FILL_SLOTS[0]))
             for what, args in events.get(s, ()):
                 what(*args)
-            if s >= len(slots) - 4 and s % 2 == 0:
-                merge((s - len(slots) + 4) // 2)
         assert not squares
         fill(len(fillers))
         stats2()
@@ -405,7 +424,8 @@ def tile_customloss_kernel(tc, cluster1, cluster2, out):
                 op=ALU.max,
             )
 
-        last = [(jt, ib) for b in (2, 0) for jt in (NT2 - 2, NT2 - 1) for ib in (b, b + 1)]
+        first = 0 if LANE_ITEMS % NCH1 == 0 else 2
+        last = [(jt, ib) for b in (first, 2 - first) for jt in (NT2 - 2, NT2 - 1) for ib in (b, b + 1)]
         banks = [multiply(jt, ib, ps_mx, "mx") for jt, ib in last[0:4]]
         for i in range(8):
             jt, ib = last[i]
@@ -413,17 +433,19 @@ def tile_customloss_kernel(tc, cluster1, cluster2, out):
             if i + 4 < 8:
                 banks.append(multiply(last[i + 4][0], last[i + 4][1], ps_mx, "mx"))
             if i == 1:
-                merge(2)
-                merge(3)
+                merge(first)
+                merge(first + 1)
             if i == 3:
-                flip_out(2)
-                flip_out(3)
+                flip_out(first)
+                flip_out(first + 1)
             if i == 5:
-                reduce_block(2)
+                merge(2 - first)
+                merge(3 - first)
+                reduce_block(first)
             if i == 6:
-                flip_out(0)
-        flip_out(1)
-        for ib in (3, 0, 1):
+                flip_out(2 - first)
+        flip_out(3 - first)
+        for ib in (first + 1, 2 - first, 3 - first):
             reduce_block(ib)
 
         fin = ps_tp.tile([P, 32], F32, tag="tp", name="fin")

@@ -30,9 +30,12 @@ RELU_AT = 4
 LIFT_AT = 2
 LANE_START = 12
 LANE_ROW = 18
+FLOOR_SLOT = 1
+HEAD_FILL = 0
+TAIL_FILL = 0
 FILL_SLOTS = (13, 89)
 DEVIATION_SLOTS = (41, 85)
-WARM = (5, 1, 1, 1, 1, 1)
+QUANTISE_LAG = 3
 FLIP_EVERY = 4
 
 
@@ -65,14 +68,11 @@ def tile_customloss_kernel(tc, cluster1, cluster2, out):
         negm1 = keep.tile([P, 4], F32)
         dev = keep.tile([P, 2, 4], F32)
         junkd = keep.tile([P, 1024], BF16)
-        sum_b = keep.tile([P, 1], F32)
-        var = keep.tile([P, 4], F32)
         m2 = keep.tile([P, 4], F32)
-        diff = keep.tile([P, 4], F32)
-        parts = keep.tile([P, 4], F32)
-        junks = keep.tile([P, 4], F32)
-        sum_a = keep.tile([P, 1], F32)
-        rest = keep.tile([P, 1], F32)
+        slack = keep.tile([P, 4], F32)
+        m1sq = keep.tile([P, 4], F32)
+        terms = keep.tile([P, 8], F32)
+        junks = keep.tile([P, 8], F32)
         res = keep.tile([P, 1], F32)
         acc_y = keep.tile([P, N1], F32)
         fmin = keep.tile([P, NCH1], F32)
@@ -169,21 +169,38 @@ def tile_customloss_kernel(tc, cluster1, cluster2, out):
 
         def stats2():
             assert pos[0] == len(fillers)
-            nc.gpsimd.tensor_tensor(out=diff[:], in0=m1[:], in1=m2[:], op=ALU.subtract)
-            nc.gpsimd.tensor_tensor(out=var[:], in0=dev[:, 0, :], in1=dev[:, 1, :], op=ALU.add)
-            nc.scalar.activation(out=junks[:], in_=var[:], func=ACT.Copy, scale=1.0 / N1, accum_out=parts[:, 2:3])
-            nc.scalar.activation(out=junks[:], in_=m1[:], func=ACT.Square, accum_out=parts[:, 3:4])
-            nc.scalar.activation(out=junks[:], in_=diff[:], func=ACT.Square, accum_out=parts[:, 0:1])
+            for w in range(4):
+                nc.scalar.activation(
+                    out=terms[:, w : w + 1],
+                    in_=m2[:, w : w + 1],
+                    func=ACT.Square,
+                    bias=m1[:, w : w + 1],
+                    scale=-1.0,
+                )
             nc.scalar.activation(
-                out=junks[:], in_=var[:], func=ACT.Relu, bias=0.1, scale=-1.0 / N1, accum_out=parts[:, 1:2]
+                out=junks[:], in_=terms[:], func=ACT.Copy, scale=-0.5 * N1 / D, accum_out=ends[:, NT1 : NT1 + 1]
             )
-            nc.gpsimd.tensor_tensor(out=sum_a[:], in0=parts[:, 0:1], in1=parts[:, 1:2], op=ALU.add)
-            nc.gpsimd.tensor_tensor(out=sum_b[:], in0=parts[:, 2:3], in1=parts[:, 3:4], op=ALU.add)
-            nc.gpsimd.tensor_scalar(
-                out=rest[:], in0=sum_a[:], scalar1=1.0 / D, scalar2=sum_b[:, 0:1], op0=ALU.mult, op1=ALU.add
+
+        def stats1():
+            nc.scalar.activation(out=slack[:], in_=dev[:, 0, :], func=ACT.Identity, bias=0.1, scale=-1.0 / N1)
+            for w in range(4):
+                nc.scalar.activation(
+                    out=terms[:, 4 + w : 5 + w],
+                    in_=dev[:, 1, w : w + 1],
+                    func=ACT.Relu,
+                    bias=slack[:, w : w + 1],
+                    scale=-1.0 / N1,
+                )
+            nc.scalar.activation(
+                out=junks[:],
+                in_=dev[:].rearrange("p h w -> p (h w)"),
+                func=ACT.Copy,
+                scale=-0.5,
+                accum_out=ends[:, NT1 + 1 : NT1 + 2],
             )
-            nc.gpsimd.tensor_scalar(
-                out=ends[:, NT1 : NT1 + 1], in0=rest[:], scalar1=-0.5 * N1, scalar2=0.0, op0=ALU.mult, op1=ALU.add
+            nc.scalar.activation(out=m1sq[:], in_=m1[:], func=ACT.Square)
+            nc.scalar.activation(
+                out=junks[:, 0:4], in_=m1sq[:], func=ACT.Copy, scale=-0.5 * N1, accum_out=ends[:, NT1 + 2 : NT1 + 3]
             )
 
         hold = [0]
@@ -283,41 +300,31 @@ def tile_customloss_kernel(tc, cluster1, cluster2, out):
 
         def pair(jt, ib):
             fold(multiply(jt, ib, ps_mx, "mx"), jt, ib)
+            if jt < 2:
+                fill(pos[0] + HEAD_FILL)
 
-        warm = keep.tile([P, 512], BF16)
-        nc.vector.memset(warm[:], 0.0)
-        idle = ps_sm.tile([P, 512], F32, tag="sums", name="idle")
-
-        def keep_warm(n):
-            for rep in range(n):
-                nc.tensor.matmul(out=idle[:], lhsT=warm[:, 0:P], rhs=warm[:], start=True, stop=True)
-
-        keep_warm(WARM[0])
         flip_in(side1, 0, 0, True)
-        keep_warm(WARM[1])
         flip_in(side1, 0, 1, True)
-        keep_warm(WARM[2])
         flip_in(side2, 0, 0, False)
-        keep_warm(WARM[3])
         quantise(side1, 0, CH)
         quantise(side2, 0, 256)
         square(0)
         flip_in(side1, 1, 0, True)
         flip_in(side1, 1, 1, False)
-        keep_warm(WARM[4])
         pair(0, 0)
         quantise(side1, CH, CH)
         square(1)
         flip_in(side1, 2, 0, False)
         flip_in(side1, 2, 1, False)
-        keep_warm(WARM[5])
         pair(1, 0)
         quantise(side1, 2 * CH, CH)
         pair(0, 1)
+        square(2)
         flip_in(side1, 3, 0, False)
         flip_in(side1, 3, 1, False)
         pair(1, 1)
         quantise(side1, 3 * CH, CH)
+        square(3)
         flip_in(side2, 0, 1, False)
         pair(0, 2)
         flip_in(side2, 1, 0, False)
@@ -325,8 +332,6 @@ def tile_customloss_kernel(tc, cluster1, cluster2, out):
         quantise(side2, 256, 256)
         pair(0, 3)
         flip_in(side2, 1, 1, False)
-        square(2)
-        square(3)
         pair(1, 3)
         nc.vector.tensor_reduce(out=flo[:], in_=fmin[:], axis=AX.X, op=ALU.min)
         quantise(side2, CH, CH)
@@ -384,7 +389,12 @@ def tile_customloss_kernel(tc, cluster1, cluster2, out):
         need[NT2 - 1] = len(slots) - 4
         flips = {FLIP_EVERY * (c - 2) // 2: c for c in range(2, NCH2)}
         for s in flips:
-            at(s + 3, quantise, side2, CH * flips[s], CH)
+            at(s + QUANTISE_LAG, quantise, side2, CH * flips[s], CH)
+        filled = pos[0]
+
+        def fill_target(s):
+            return filled + (len(fillers) - filled) * (s - FILL_SLOTS[0]) // (FILL_SLOTS[1] - FILL_SLOTS[0])
+
         squares = sorted([(need[t], t) for t in need if t not in ready])
         spread = None
         for s in range(len(slots)):
@@ -395,16 +405,18 @@ def tile_customloss_kernel(tc, cluster1, cluster2, out):
             while squares and squares[0][0] <= s:
                 square(squares.pop(0)[1])
             pair(jt, ib)
-            if s == 1:
+            if s == FLOOR_SLOT:
                 spread = find_floor()
-            if s == 3:
+            if s == FLOOR_SLOT + 2:
                 nc.vector.tensor_reduce(out=negf[:], in_=spread[:, 0:P], axis=AX.X, op=ALU.max, negate=True)
-            fill(len(fillers) * (s - FILL_SLOTS[0]) // (FILL_SLOTS[1] - FILL_SLOTS[0]))
+            fill(fill_target(s))
             for what, args in events.get(s, ()):
                 what(*args)
         assert not squares
-        fill(len(fillers))
-        stats2()
+        for s in sorted(events):
+            if s >= len(slots):
+                for what, args in events[s]:
+                    what(*args)
 
         flipped = {}
 
@@ -424,28 +436,25 @@ def tile_customloss_kernel(tc, cluster1, cluster2, out):
                 op=ALU.max,
             )
 
-        first = 0 if LANE_ITEMS % NCH1 == 0 else 2
-        last = [(jt, ib) for b in (first, 2 - first) for jt in (NT2 - 2, NT2 - 1) for ib in (b, b + 1)]
+        last = [(jt, ib) for jt in (NT2 - 2, NT2 - 1) for ib in range(NCH1)]
         banks = [multiply(jt, ib, ps_mx, "mx") for jt, ib in last[0:4]]
         for i in range(8):
             jt, ib = last[i]
             fold(banks[i], jt, ib)
+            fill(fill_target(len(slots) + i))
+            if i == TAIL_FILL:
+                fill(len(fillers))
+                stats1()
+                stats2()
             if i + 4 < 8:
                 banks.append(multiply(last[i + 4][0], last[i + 4][1], ps_mx, "mx"))
-            if i == 1:
-                merge(first)
-                merge(first + 1)
-            if i == 3:
-                flip_out(first)
-                flip_out(first + 1)
-            if i == 5:
-                merge(2 - first)
-                merge(3 - first)
-                reduce_block(first)
-            if i == 6:
-                flip_out(2 - first)
-        flip_out(3 - first)
-        for ib in (first + 1, 2 - first, 3 - first):
+            if i >= 5:
+                merge(i - 5)
+                flip_out(i - 5)
+        reduce_block(0)
+        merge(3)
+        flip_out(3)
+        for ib in range(1, NCH1):
             reduce_block(ib)
 
         fin = ps_tp.tile([P, 32], F32, tag="tp", name="fin")

import math
from contextlib import ExitStack

import concourse.mybir as mybir
from concourse.masks import make_identity

F32 = mybir.dt.float32
BF16 = mybir.dt.bfloat16
U32 = mybir.dt.uint32
U8 = mybir.dt.uint8
FP8X4 = mybir.dt.float8_e4m3fn_x4
ALU = mybir.AluOpType
ACT = mybir.ActivationFunctionType
AX = mybir.AxisListType

P = 128
N1, N2, D = 2048, 4096, 512
CH = 512
TPC = CH // P
NCH1 = N1 // CH
NCH2 = N2 // CH
NT1 = N1 // P
NT2 = N2 // P
FLOPS = 2 * N1 * N2 * D
LANE0 = 4
LANE_ITEMS = 20
SQ_MARGIN = 10
SQ_FROM = 12
RELU_AT = 4
LIFT_AT = 2
LANE_START = 12
LANE_ROW = 18
FLOOR_SLOT = 1
HEAD_FILL = 0
TAIL_FILL = 0
FILL_SLOTS = (13, 89)
DEVIATION_SLOTS = (41, 85)
QUANTISE_LAG = 3
FLIP_EVERY = 4


def tile_customloss_kernel(tc, cluster1, cluster2, out):
    nc = tc.nc
    with ExitStack() as ctx:
        keep = ctx.enter_context(tc.tile_pool(name="keep", bufs=1))
        scrap = ctx.enter_context(tc.tile_pool(name="scrap", bufs=2))
        side_pool = ctx.enter_context(tc.tile_pool(name="side_pool", bufs=2))
        ps_tp = ctx.enter_context(tc.psum_pool(name="ps_tp", bufs=3))
        ps_mx = ctx.enter_context(tc.psum_pool(name="ps_mx", bufs=4))
        ps_sm = ctx.enter_context(tc.psum_pool(name="ps_sm", bufs=1))
        ctx.enter_context(tc.manual_schedule())

        x1 = keep.tile([P, NT1, D], BF16)
        x2 = keep.tile([P, NT2, D], BF16)
        g1 = keep.tile([P, N1, 4], BF16, align_bytes=64)
        g2 = keep.tile([P, N2, 4], BF16, align_bytes=64)
        codes1 = keep.tile([P, N1], U32, align_bytes=64)
        codes2 = keep.tile([P, N2], U32, align_bytes=64)
        scales1 = keep.tile([P, N1], U8, align_bytes=64)
        scales2 = keep.tile([P, N2], U8, align_bytes=64)
        acc = keep.tile([P, N1], F32)
        ident = keep.tile([P, P], F32)
        ones = keep.tile([P, 2], BF16)
        half2 = keep.tile([P, NT2], F32)
        ends = keep.tile([P, 32], F32)
        weight = keep.tile([P, P], F32)
        m1 = keep.tile([P, 4], F32)
        negm1 = keep.tile([P, 4], F32)
        dev = keep.tile([P, 2, 4], F32)
        junkd = keep.tile([P, 1024], BF16)
        m2 = keep.tile([P, 4], F32)
        slack = keep.tile([P, 4], F32)
        m1sq = keep.tile([P, 4], F32)
        terms = keep.tile([P, 8], F32)
        junks = keep.tile([P, 8], F32)
        res = keep.tile([P, 1], F32)
        acc_y = keep.tile([P, N1], F32)
        fmin = keep.tile([P, NCH1], F32)
        flo = keep.tile([P, 1], F32)
        negf = keep.tile([P, 1], F32)
        negb = keep.tile([P, NT2], F32)

        make_identity(nc, ident[:])
        nc.vector.memset(ones[:], 1.0)
        nc.vector.memset(ends[:], 0.0)
        nc.vector.memset(weight[:], -2.0 / N1)

        def load(x, src, t0, nt):
            nc.sync.dma_start(
                out=x[:, t0 : t0 + nt, :],
                in_=src[P * t0 : P * (t0 + nt), :].rearrange("(p t) k -> p t k", t=nt),
            )

        load(x1, cluster1, 0, 2)
        load(x1, cluster1, 2, 2)
        load(x2, cluster2, 0, 2)
        for c in range(1, NCH1):
            load(x1, cluster1, TPC * c, TPC)
        load(x2, cluster2, 2, 2)
        for c in range(1, NCH2):
            load(x2, cluster2, TPC * c, TPC)

        side1 = (x1, g1, codes1, scales1)
        side2 = (x2, g2, codes2, scales2)

        def flip_in(side, c, b, on_vector):
            x, g = side[0], side[1]
            xf = x[:].bitcast(F32)
            gf = g[:].bitcast(F32)
            tp = ps_tp.tile([P, 512], F32, tag="tp", name="tp")
            tpv = tp[:].rearrange("p (u r) -> p u r", u=2)
            for s in range(2):
                for u in range(2):
                    nc.tensor.transpose(
                        tpv[:, u, P * s : P * (s + 1)],
                        xf[:, TPC * c + 2 * b + s, P * u : P * (u + 1)],
                        ident[:],
                    )
            r0 = CH * c + 256 * b
            dst = gf[:, r0 : r0 + 256, :]
            src = tp[:].rearrange("p (u r) -> p r u", u=2)
            if on_vector:
                nc.vector.tensor_copy(out=dst, in_=src)
            else:
                nc.scalar.copy(out=dst, in_=src)

        def quantise(side, r0, nrows):
            g, codes, scales = side[1], side[2], side[3]
            rows = slice(r0, r0 + nrows)
            nc.vector.quantize_mx(
                out=codes[:, rows].bitcast(FP8X4),
                scales=scales[:, rows],
                in_=g[:, rows, :].rearrange("p r t -> p (r t)"),
            )

        ready = set()

        def square(t):
            junk = scrap.tile([P, D], BF16, tag="junk")
            nc.scalar.activation(
                out=junk[:], in_=x2[:, t, :], func=ACT.Square, scale=math.sqrt(0.5), accum_out=half2[:, t : t + 1]
            )
            ready.add(t)

        fillers = []
        for kind, x, ntiles in (("sum1", x1, NT1), ("sum2", x2, NT2)):
            for w in range(4):
                for t in range(ntiles):
                    fillers.append((kind, x, ntiles, w, t))
        pos = [0]
        bank = {}

        def finish(kind):
            if kind == "sum1":
                nc.scalar.activation(out=m1[:], in_=bank[kind][:, 0:8:2], func=ACT.Copy, scale=1.0 / N1)
                nc.scalar.activation(out=negm1[:], in_=bank[kind][:, 0:8:2], func=ACT.Copy, scale=-1.0 / N1)
            else:
                nc.scalar.activation(out=m2[:], in_=bank[kind][:, 0:8:2], func=ACT.Copy, scale=1.0 / N2)

        def deviation(w, h):
            nc.scalar.activation(
                out=junkd[:],
                in_=g1[:, 1024 * h : 1024 * (h + 1), w],
                func=ACT.Square,
                bias=negm1[:, w : w + 1],
                scale=1.0,
                accum_out=dev[:, h, w : w + 1],
            )

        def stats2():
            assert pos[0] == len(fillers)
            for w in range(4):
                nc.scalar.activation(
                    out=terms[:, w : w + 1],
                    in_=m2[:, w : w + 1],
                    func=ACT.Square,
                    bias=m1[:, w : w + 1],
                    scale=-1.0,
                )
            nc.scalar.activation(
                out=junks[:], in_=terms[:], func=ACT.Copy, scale=-0.5 * N1 / D, accum_out=ends[:, NT1 : NT1 + 1]
            )

        def stats1():
            nc.scalar.activation(out=slack[:], in_=dev[:, 0, :], func=ACT.Identity, bias=0.1, scale=-1.0 / N1)
            for w in range(4):
                nc.scalar.activation(
                    out=terms[:, 4 + w : 5 + w],
                    in_=dev[:, 1, w : w + 1],
                    func=ACT.Relu,
                    bias=slack[:, w : w + 1],
                    scale=-1.0 / N1,
                )
            nc.scalar.activation(
                out=junks[:],
                in_=dev[:].rearrange("p h w -> p (h w)"),
                func=ACT.Copy,
                scale=-0.5,
                accum_out=ends[:, NT1 + 1 : NT1 + 2],
            )
            nc.scalar.activation(out=m1sq[:], in_=m1[:], func=ACT.Square)
            nc.scalar.activation(
                out=junks[:, 0:4], in_=m1sq[:], func=ACT.Copy, scale=-0.5 * N1, accum_out=ends[:, NT1 + 2 : NT1 + 3]
            )

        hold = [0]

        def fill(target):
            if hold[0] > 0:
                hold[0] -= 1
                return
            while pos[0] < min(target, len(fillers)):
                kind, x, ntiles, w, t = fillers[pos[0]]
                pos[0] += 1
                if w == 0 and t == 0:
                    bank[kind] = ps_sm.tile([P, 512], F32, tag="sums", name="sums")
                block = x[:, t, :].rearrange("p (u q e) -> p u e q", u=2, e=2)[:, w // 2, w % 2, :]
                dst = bank[kind][:, 2 * w : 2 * w + 2]
                nc.tensor.matmul(out=dst, lhsT=block, rhs=ones[:], start=(t == 0), stop=(t == ntiles - 1))
                if w == 3 and t == ntiles - 1:
                    finish(kind)
                    hold[0] = 2
                    return

        started = set()

        def multiply(jt, ib, pool, tag):
            ps = pool.tile([P, 512], F32, tag=tag, name="mx")
            jc = slice(P * jt, P * (jt + 1))
            ic = slice(512 * ib, 512 * (ib + 1))
            nc.tensor.matmul_mx(
                out=ps[:],
                lhsT=codes2[:, jc].bitcast(FP8X4),
                lhsT_scale=scales2[:, jc],
                rhs=codes1[:, ic].bitcast(FP8X4),
                rhs_scale=scales1[:, ic],
                start=True,
                stop=True,
            )
            return ps

        def fold(ps, jt, ib):
            assert jt in ready
            ic = slice(512 * ib, 512 * (ib + 1))
            if ib in started:
                nc.vector.scalar_tensor_tensor(
                    out=acc[:, ic],
                    in0=ps[:],
                    scalar=half2[:, jt : jt + 1],
                    in1=acc[:, ic],
                    op0=ALU.subtract,
                    op1=ALU.max,
                )
            else:
                started.add(ib)
                nc.vector.tensor_scalar(
                    out=acc[:, ic],
                    in0=ps[:],
                    scalar1=half2[:, jt : jt + 1],
                    scalar2=None,
                    op0=ALU.subtract,
                    op1=ALU.min,
                    accum_out=fmin[:, ib : ib + 1],
                )

        lane = {}

        def lift(k):
            jt, ib = LANE0 + k // NCH1, k % NCH1
            assert jt in ready
            ps = multiply(jt, ib, ps_tp, "tp")
            if ib == 0:
                nc.scalar.activation(
                    out=negb[:, jt : jt + 1],
                    in_=half2[:, jt : jt + 1],
                    func=ACT.Identity,
                    bias=negf[:, 0:1],
                    scale=-1.0,
                )
            n, h = k // NCH1, ib // 2
            if n == 0:
                dst = acc_y[:, 512 * ib : 512 * (ib + 1)]
            else:
                if ib % 2 == 0:
                    lane[n, h] = side_pool.tile([P, 1024], F32, tag="ys%d" % h, name="ys")
                dst = lane[n, h][:, 512 * (ib % 2) : 512 * (ib % 2 + 1)]
            nc.scalar.activation(out=dst, in_=ps[:], func=ACT.Relu, bias=negb[:, jt : jt + 1], scale=1.0)

        def gain(n, h):
            ys = lane[n, h]
            nc.gpsimd.tensor_tensor(
                out=ys[:], in0=ys[:], in1=acc_y[:, 1024 * h : 1024 * (h + 1)], op=ALU.subtract
            )

        def raise_maximum(n, h):
            ys = lane[n, h]
            best = acc_y[:, 1024 * h : 1024 * (h + 1)]
            nc.scalar.activation(out=ys[:], in_=ys[:], func=ACT.Relu)
            nc.gpsimd.tensor_tensor(out=best, in0=best, in1=ys[:], op=ALU.add)

        def pair(jt, ib):
            fold(multiply(jt, ib, ps_mx, "mx"), jt, ib)
            if jt < 2:
                fill(pos[0] + HEAD_FILL)

        flip_in(side1, 0, 0, True)
        flip_in(side1, 0, 1, True)
        flip_in(side2, 0, 0, False)
        quantise(side1, 0, CH)
        quantise(side2, 0, 256)
        square(0)
        flip_in(side1, 1, 0, True)
        flip_in(side1, 1, 1, False)
        pair(0, 0)
        quantise(side1, CH, CH)
        square(1)
        flip_in(side1, 2, 0, False)
        flip_in(side1, 2, 1, False)
        pair(1, 0)
        quantise(side1, 2 * CH, CH)
        pair(0, 1)
        square(2)
        flip_in(side1, 3, 0, False)
        flip_in(side1, 3, 1, False)
        pair(1, 1)
        quantise(side1, 3 * CH, CH)
        square(3)
        flip_in(side2, 0, 1, False)
        pair(0, 2)
        flip_in(side2, 1, 0, False)
        pair(1, 2)
        quantise(side2, 256, 256)
        pair(0, 3)
        flip_in(side2, 1, 1, False)
        pair(1, 3)
        nc.vector.tensor_reduce(out=flo[:], in_=fmin[:], axis=AX.X, op=ALU.min)
        quantise(side2, CH, CH)

        def find_floor():
            spread = ps_sm.tile([P, 512], F32, tag="sums", name="spread")
            nc.tensor.matmul(
                out=spread[:, 0:P], lhsT=flo[:, 0:1].to_broadcast([P, P]), rhs=ident[:], start=True, stop=True
            )
            return spread

        def merge(ib):
            ic = slice(512 * ib, 512 * (ib + 1))
            nc.vector.scalar_tensor_tensor(
                out=acc[:, ic],
                in0=acc_y[:, ic],
                scalar=negf[:, 0:1],
                in1=acc[:, ic],
                op0=ALU.subtract,
                op1=ALU.max,
            )

        in_lane = {(LANE0 + k // NCH1, k % NCH1) for k in range(LANE_ITEMS)}
        slots = [(jt, ib) for jt in range(2, NT2 - 2) for ib in range(NCH1) if (jt, ib) not in in_lane]
        events = {}

        def at(slot, what, *args):
            events.setdefault(slot, []).append((what, args))

        first_row = LANE_START + 4
        for i in range(8):
            n, h = (i // 2) % 2, i // 4
            at(LANE_START + i, lift, NCH1 * n + 2 * h + i % 2)
        n_rows = (LANE_ITEMS - 1) // NCH1
        for n in range(1, n_rows + 1):
            base = first_row + LANE_ROW * (n - 1)
            for h in range(2):
                if NCH1 * n + 2 * h < LANE_ITEMS:
                    at(base + LANE_ROW * h // 4, gain, n, h)
                    at(base + LANE_ROW * (RELU_AT + 3 * h) // 12, raise_maximum, n, h)
            for i in range(4):
                if NCH1 * (n + 1) + i < LANE_ITEMS:
                    at(base + LANE_ROW * (2 * i + LIFT_AT) // 8, lift, NCH1 * (n + 1) + i)
        for i in range(8):
            at(DEVIATION_SLOTS[0] + i * (DEVIATION_SLOTS[1] - DEVIATION_SLOTS[0]) // 8, deviation, i // 2, i % 2)
        need = {}
        for s in range(len(slots)):
            need.setdefault(slots[s][0], max(s - SQ_MARGIN, min(s - 5, SQ_FROM), 0))
        for slot in events:
            for what, args in events[slot]:
                if what is lift and args[0] % NCH1 == 0:
                    jt = LANE0 + args[0] // NCH1
                    need[jt] = min(need.get(jt, 999), slot - 1)
        need[NT2 - 2] = len(slots) - 6
        need[NT2 - 1] = len(slots) - 4
        flips = {FLIP_EVERY * (c - 2) // 2: c for c in range(2, NCH2)}
        for s in flips:
            at(s + QUANTISE_LAG, quantise, side2, CH * flips[s], CH)
        filled = pos[0]

        def fill_target(s):
            return filled + (len(fillers) - filled) * (s - FILL_SLOTS[0]) // (FILL_SLOTS[1] - FILL_SLOTS[0])

        squares = sorted([(need[t], t) for t in need if t not in ready])
        spread = None
        for s in range(len(slots)):
            jt, ib = slots[s]
            if s in flips:
                flip_in(side2, flips[s], 0, False)
                flip_in(side2, flips[s], 1, False)
            while squares and squares[0][0] <= s:
                square(squares.pop(0)[1])
            pair(jt, ib)
            if s == FLOOR_SLOT:
                spread = find_floor()
            if s == FLOOR_SLOT + 2:
                nc.vector.tensor_reduce(out=negf[:], in_=spread[:, 0:P], axis=AX.X, op=ALU.max, negate=True)
            fill(fill_target(s))
            for what, args in events.get(s, ()):
                what(*args)
        assert not squares
        for s in sorted(events):
            if s >= len(slots):
                for what, args in events[s]:
                    what(*args)

        flipped = {}

        def flip_out(ib):
            ft = ps_tp.tile([P, 512], F32, tag="tp", name="ft")
            for q in range(4):
                nc.tensor.transpose(
                    ft[:, P * q : P * (q + 1)], acc[:, 512 * ib + P * q : 512 * ib + P * (q + 1)], ident[:]
                )
            flipped[ib] = ft

        def reduce_block(ib):
            nc.vector.tensor_reduce(
                out=ends[:, 4 * ib : 4 * (ib + 1)],
                in_=flipped[ib][:].rearrange("p (c j) -> p c j", c=4),
                axis=AX.X,
                op=ALU.max,
            )

        last = [(jt, ib) for jt in (NT2 - 2, NT2 - 1) for ib in range(NCH1)]
        banks = [multiply(jt, ib, ps_mx, "mx") for jt, ib in last[0:4]]
        for i in range(8):
            jt, ib = last[i]
            fold(banks[i], jt, ib)
            fill(fill_target(len(slots) + i))
            if i == TAIL_FILL:
                fill(len(fillers))
                stats1()
                stats2()
            if i + 4 < 8:
                banks.append(multiply(last[i + 4][0], last[i + 4][1], ps_mx, "mx"))
            if i >= 5:
                merge(i - 5)
                flip_out(i - 5)
        reduce_block(0)
        merge(3)
        flip_out(3)
        for ib in range(1, NCH1):
            reduce_block(ib)

        fin = ps_tp.tile([P, 32], F32, tag="tp", name="fin")
        nc.tensor.matmul(out=fin[:], lhsT=weight[:], rhs=ends[:], start=True, stop=True)
        nc.vector.tensor_reduce(out=res[:], in_=fin[:], axis=AX.X, op=ALU.add)

        out_view = out
        for extra in range(2 - out.ndim):
            out_view = out_view.unsqueeze(0)
        nc.sync.dma_start(out=out_view, in_=res[0:1, 0:1])
